import numpy as np
import ml_dtypes


def mxq(x, axis, fmt="e4m3"):
    dtype, down = {"e4m3": (ml_dtypes.float8_e4m3fn, 7), "e5m2": (ml_dtypes.float8_e5m2, 14)}[fmt]
    v = np.moveaxis(np.asarray(x, np.float32).astype(ml_dtypes.bfloat16).astype(np.float64), axis, -1)
    blocks = v.reshape(v.shape[:-1] + (-1, 32))
    amax = np.abs(blocks).max(-1, keepdims=True)
    byte = np.maximum(np.where(amax > 0, np.frexp(amax)[1] - 1 + 127, 0) - down, 1)
    scale = np.exp2(byte - 127.0)
    codes = (blocks / scale).astype(np.float32).astype(dtype).astype(np.float64)
    return np.moveaxis((codes * scale).reshape(v.shape), -1, axis)


WIDE = False


def mx_kscale(k):
    if not WIDE:
        return np.ones(k)
    levels = np.array([10, -10, 5, -5, 0])
    a = np.random.permutation(np.resize(levels, k // 512 * 4)).reshape(k // 512, 4)
    idx = np.arange(k)
    return np.exp2(a[idx // 512, idx % 128 // 32])


BF16 = ml_dtypes.bfloat16


def bf(x):
    return np.asarray(x, np.float32).astype(BF16)


def f64(x):
    return np.asarray(x).astype(np.float64)


E2M1 = np.array([0.0, 0.5, 1.0, 1.5, 2.0, 3.0, 4.0, 6.0, -0.0, -0.5, -1.0, -1.5, -2.0, -3.0, -4.0, -6.0])


def pack_weight(w, fmt):
    k, n = w.shape
    w = f64(bf(w)).reshape(k // 32, 32, n)
    amax = np.abs(w).max(1)
    if fmt == "e4m3":
        byte = np.frexp(amax)[1] - 1 + 127 - 7
    else:
        mant, ex = np.frexp(amax / 6.0)
        byte = np.where(mant > 0.5, ex, ex - 1) + 127
    byte = np.clip(np.where(amax > 0, byte, 1), 1, 254)
    scaled = (w * np.exp2(127.0 - byte)[:, None, :]).reshape(k, n).astype(np.float32)
    by_word = np.ascontiguousarray(scaled.reshape(k // 512, 128, 4, n).transpose(0, 1, 3, 2))
    if fmt == "e4m3":
        words = by_word.astype(ml_dtypes.float8_e4m3fn).view(np.uint8)
    else:
        c = by_word.astype(ml_dtypes.float4_e2m1fn).view(np.uint8) & 0xF
        words = c[..., 0::2] | (c[..., 1::2] << 4)
    return np.ascontiguousarray(words), np.ascontiguousarray(byte.astype(np.uint8).reshape(k // 512, 16, n))


def unpack_weight(words, scales, fmt):
    g, p, n, _ = words.shape
    if fmt == "e4m3":
        vals = np.ascontiguousarray(words).view(ml_dtypes.float8_e4m3fn).astype(np.float64)
    else:
        nib = np.empty((g, p, n, 4), np.uint8)
        nib[..., 0::2] = words & 0xF
        nib[..., 1::2] = words >> 4
        vals = E2M1[nib]
    vals = vals * np.repeat(np.exp2(scales.astype(np.float64) - 127.0), 8, axis=1)[..., None]
    return vals.transpose(0, 1, 3, 2).reshape(g * 512, n)

def pack4(w):
    words, scales = pack_weight(w, "e2m1")
    return words.reshape(words.shape[0], 128, -1), scales


def unpack4(words, scales):
    return unpack_weight(words.reshape(words.shape[0], 128, -1, 2), scales, "e2m1")


B, IN, H, NS, SS, CS, NA = 1024, 256, 2048, 4, 8, 128, 3
NC = NS * CS


def setup_inputs():
    s = mx_kscale(H)
    h = bf(np.tanh(np.random.standard_normal((B, H))) * s)
    act_logits = bf(np.random.standard_normal((B, NS * NA)) * 1.5)
    stacks = bf(np.random.standard_normal((B, NS, SS, CS)) * 1.5)
    W_push = np.random.standard_normal((NC, H)) * 5.0 / np.sqrt(H) / s
    W_push_words, W_push_scales = pack4(np.ascontiguousarray(W_push.T))
    b_push = bf(np.random.standard_normal(NC) * 0.7)
    return {
        "h": h,
        "act_logits": act_logits,
        "stacks": stacks,
        "W_push_words": W_push_words,
        "W_push_scales": W_push_scales,
        "b_push": b_push,
    }


def reference(h, act_logits, stacks, W_push_words, W_push_scales, b_push):
    st = f64(stacks)
    push = ((mxq(f64(h), 1, "e4m3") @ unpack4(W_push_words, W_push_scales)) + f64(b_push)).reshape(B, NS, CS)
    lg = f64(act_logits)
    e = np.exp(lg - lg.max(-1, keepdims=True))
    act = (e / e.sum(-1, keepdims=True)).reshape(B, NS, NA)
    pa, po, no = act[..., 0][..., None], act[..., 1][..., None], act[..., 2][..., None]
    top_new = pa * push + po * st[:, :, 1, :] + no * st[:, :, 0, :]
    zeros_tail = np.zeros((B, NS, 1, CS))
    pop_rest = np.concatenate([st[:, :, 2:, :], zeros_tail], axis=2)
    rest = (pa[:, :, :, None] * st[:, :, :-1, :]
            + po[:, :, :, None] * pop_rest
            + no[:, :, :, None] * st[:, :, 1:, :])
    return np.concatenate([top_new[:, :, None, :], rest], axis=2)

@@ -1,0 +1,204 @@
+from contextlib import ExitStack
+
+import concourse.mybir as mybir
+from concourse.masks import make_identity
+
+F32 = mybir.dt.float32
+BF16 = mybir.dt.bfloat16
+U8 = mybir.dt.uint8
+U32 = mybir.dt.uint32
+I32 = mybir.dt.int32
+FP8X4 = mybir.dt.float8_e4m3fn_x4
+FP4X4 = mybir.dt.float4_e2m1fn_x4
+ACT = mybir.ActivationFunctionType
+ALU = mybir.AluOpType
+AXIS_X = mybir.AxisListType.X
+
+P = 128
+B = 1024
+H = 2048
+STACKS = 4
+CELLS = 8
+CELL = 128
+ACTIONS = 3
+DEPTH = CELLS * CELL
+TILES = B // P
+PASSES = H // 512
+WORDS = 256
+
+FLOPS = 2 * B * H * STACKS * CELL
+
+
+def tile_stackrnncore_pa_kernel(tc, h, act_logits, stacks, W_push_words, W_push_scales, b_push, out):
+    nc = tc.nc
+    h_rows = h.rearrange("(p t) k -> p t k", t=TILES)
+    stack_rows = stacks.rearrange("(p t) n i c -> p t n (i c)", t=TILES)
+    out_rows = out.rearrange("(p t) n i c -> p t n (i c)", t=TILES)
+
+    with ExitStack() as ctx:
+        keep = ctx.enter_context(tc.tile_pool(name="keep", bufs=1))
+        stage = ctx.enter_context(tc.tile_pool(name="stage", bufs=2))
+        blend = ctx.enter_context(tc.tile_pool(name="blend", bufs=4))
+        psum = ctx.enter_context(tc.psum_pool(name="psum", bufs=2))
+        psum_once = ctx.enter_context(tc.psum_pool(name="psum_once", bufs=1))
+        ctx.enter_context(tc.manual_schedule())
+
+        zero = keep.tile([P, 1], F32)
+        nc.gpsimd.memset(zero[:], 0.0)
+        one = keep.tile([P, 1], F32)
+        nc.scalar.activation(out=one[:], in_=zero[:], func=ACT.Exp)
+        ident = keep.tile([P, P], F32)
+        make_identity(nc, ident[:])
+        bias_rows = keep.tile([P, P], BF16)
+        nc.gpsimd.memset(bias_rows[:], 0.0)
+        w_scales = keep.tile([P, PASSES, STACKS * CELL], U8, align_bytes=64)
+        nc.vector.memset(w_scales[:].bitcast(I32), 0)
+
+        logits = keep.tile([P, TILES, STACKS * ACTIONS], BF16)
+        nc.sync.dma_start(out=logits[:], in_=act_logits.rearrange("(p t) a -> p t a", t=TILES))
+        stack_sb = [keep.tile([P, STACKS, DEPTH], BF16, name="stack_sb%d" % t) for t in range(TILES)]
+        h_sb = [keep.tile([P, H], BF16, name="h_sb%d" % t) for t in range(TILES)]
+        w_words = keep.tile([P, PASSES, 2 * STACKS * CELL], U8, align_bytes=64)
+        nc.sync.dma_start(out=stack_sb[0][:, 0:2, :], in_=stack_rows[:, 0, 0:2, :])
+        nc.sync.dma_start(out=bias_rows[0:STACKS, :], in_=b_push.rearrange("(n c) -> n c", n=STACKS))
+        nc.sync.dma_start(out=h_sb[0][:], in_=h_rows[:, 0, :])
+        scale_words = W_push_scales.bitcast(I32)
+        for quad in range(4):
+            nc.sync.dma_start(
+                out=w_scales[32 * quad : 32 * quad + 4, :, :].bitcast(I32),
+                in_=scale_words[:, 4 * quad : 4 * quad + 4, :].rearrange("g r w -> r g w"),
+            )
+        nc.sync.dma_start(out=w_words[:].bitcast(I32), in_=W_push_words.bitcast(I32).rearrange("g p w -> p g w"))
+        nc.sync.dma_start(out=stack_sb[0][:, 2:4, :], in_=stack_rows[:, 0, 2:4, :])
+        for t in range(1, TILES):
+            nc.sync.dma_start(out=h_sb[t][:], in_=h_rows[:, t, :])
+            nc.sync.dma_start(out=stack_sb[t][:], in_=stack_rows[:, t, :, :])
+
+        shape = [P, TILES, STACKS * ACTIONS]
+        top_logit = keep.tile([P, TILES], F32)
+        nc.vector.tensor_reduce(out=top_logit[:], in_=logits[:], axis=AXIS_X, op=ALU.max)
+        shifted = keep.tile(shape, F32)
+        nc.vector.tensor_tensor(
+            out=shifted[:], in0=logits[:], in1=top_logit[:].unsqueeze(2).to_broadcast(shape), op=ALU.subtract
+        )
+        expd = keep.tile(shape, F32)
+        nc.scalar.activation(out=expd[:], in_=shifted[:], func=ACT.Exp)
+        total = keep.tile([P, TILES], F32)
+        nc.vector.tensor_reduce(out=total[:], in_=expd[:], axis=AXIS_X, op=ALU.add)
+        inverse = keep.tile([P, TILES], F32)
+        nc.vector.reciprocal(out=inverse[:], in_=total[:])
+        weights = keep.tile(shape, F32)
+        nc.vector.tensor_tensor(
+            out=weights[:], in0=expd[:], in1=inverse[:].unsqueeze(2).to_broadcast(shape), op=ALU.mult
+        )
+
+        def weight(t, n, action):
+            column = ACTIONS * n + action
+            return weights[:, t, column : column + 1]
+
+        bias_rows_f32 = keep.tile([P, P], F32)
+        nc.gpsimd.tensor_copy(out=bias_rows_f32[:], in_=bias_rows[:])
+        bias_ps = psum_once.tile([P, P], F32)
+        nc.tensor.transpose(bias_ps[:], bias_rows_f32[:], ident[:])
+        bias_col = keep.tile([P, STACKS], F32)
+        nc.vector.tensor_copy(out=bias_col[:], in_=bias_ps[:, 0:STACKS])
+
+        def stay(t, acc, n):
+            nc.scalar.activation(out=acc[:, n, :], in_=stack_sb[t][:, n, :], func=ACT.Copy, scale=weight(t, n, 2))
+
+        def pop(t, acc, n):
+            nc.vector.scalar_tensor_tensor(
+                out=acc[:, n, 0 : DEPTH - CELL],
+                in0=stack_sb[t][:, n, CELL:DEPTH],
+                scalar=weight(t, n, 1),
+                in1=acc[:, n, 0 : DEPTH - CELL],
+                op0=ALU.mult,
+                op1=ALU.add,
+            )
+
+        def shift_down(t, acc, n):
+            nc.vector.scalar_tensor_tensor(
+                out=acc[:, n, CELL:DEPTH],
+                in0=stack_sb[t][:, n, 0 : DEPTH - CELL],
+                scalar=weight(t, n, 0),
+                in1=acc[:, n, CELL:DEPTH],
+                op0=ALU.mult,
+                op1=ALU.add,
+            )
+
+        for t in range(TILES):
+            acc = blend.tile([P, STACKS, DEPTH], F32)
+
+            h_words = h_sb[t][:].bitcast(F32)
+            turned = []
+            for half in range(2):
+                turned_ps = psum.tile([P, 4, P], F32)
+                for g in range(2):
+                    for u in range(2):
+                        k_pass = 2 * half + g
+                        nc.tensor.transpose(
+                            turned_ps[:, 2 * g + u, :],
+                            h_words[:, WORDS * k_pass + u : WORDS * (k_pass + 1) : 2],
+                            ident[:],
+                        )
+                turned.append(turned_ps)
+
+            stay(t, acc, 0)
+            stay(t, acc, 1)
+            pop(t, acc, 0)
+            pop(t, acc, 1)
+
+            grouped = stage.tile([P, H], BF16, align_bytes=64)
+            grouped_words = grouped[:].bitcast(F32).rearrange("p (g b u) -> p g b u", g=PASSES, u=2)
+            for half in range(2):
+                nc.scalar.copy(
+                    out=grouped_words[:, 2 * half : 2 * half + 2, :, :],
+                    in_=turned[half][:].rearrange("p (g u) b -> p g b u", u=2),
+                )
+            h_codes = stage.tile([P, PASSES * P], U32, align_bytes=64)
+            h_scales = stage.tile([P, PASSES * P], U8, align_bytes=64)
+            nc.vector.quantize_mx(out=h_codes[:].bitcast(FP8X4), scales=h_scales[:], in_=grouped[:])
+
+            push_t_ps = psum.tile([P, STACKS, P], F32)
+            for n in range(STACKS):
+                for g in range(PASSES):
+                    nc.tensor.matmul_mx(
+                        out=push_t_ps[:, n, :],
+                        lhsT=w_words[:, g, 2 * CELL * n : 2 * CELL * (n + 1)].bitcast(FP4X4),
+                        lhsT_scale=w_scales[:, g, CELL * n : CELL * (n + 1)],
+                        rhs=h_codes[:, P * g : P * (g + 1)].bitcast(FP8X4),
+                        rhs_scale=h_scales[:, P * g : P * (g + 1)],
+                        start=(g == 0),
+                        stop=(g == PASSES - 1),
+                    )
+
+            shift_down(t, acc, 0)
+            shift_down(t, acc, 1)
+            nc.sync.dma_start(out=out_rows[:, t, 0:2, CELL:DEPTH], in_=acc[:, 0:2, CELL:DEPTH])
+
+            stay(t, acc, 2)
+            stay(t, acc, 3)
+            pop(t, acc, 2)
+            pop(t, acc, 3)
+            shift_down(t, acc, 2)
+            shift_down(t, acc, 3)
+            nc.sync.dma_start(out=out_rows[:, t, 2:4, CELL:DEPTH], in_=acc[:, 2:4, CELL:DEPTH])
+
+            push_t = stage.tile([P, STACKS, P], F32)
+            push_ps = psum.tile([P, STACKS, CELL], F32)
+            for n in range(STACKS):
+                nc.scalar.activation(
+                    out=push_t[:, n, :], in_=push_t_ps[:, n, :], func=ACT.Identity, bias=bias_col[:, n : n + 1], scale=1.0
+                )
+            for n in range(STACKS):
+                nc.tensor.transpose(push_ps[:, n, :], push_t[:, n, :], ident[:])
+            for n in range(STACKS):
+                nc.vector.scalar_tensor_tensor(
+                    out=acc[:, n, 0:CELL],
+                    in0=push_ps[:, n, :],
+                    scalar=weight(t, n, 0),
+                    in1=acc[:, n, 0:CELL],
+                    op0=ALU.mult,
+                    op1=ALU.add,
+                )
+            nc.sync.dma_start(out=out_rows[:, t, :, 0:CELL], in_=acc[:, :, 0:CELL])

@@ -96,12 +96,54 @@ def tile_stackrnncore_pa_kernel(tc, h, act_logits, stacks, W_push_words, W_push_
             column = ACTIONS * n + action
             return weights[:, t, column : column + 1]
 
-        bias_rows_f32 = keep.tile([P, P], F32)
-        nc.gpsimd.tensor_copy(out=bias_rows_f32[:], in_=bias_rows[:])
-        bias_ps = psum_once.tile([P, P], F32)
-        nc.tensor.transpose(bias_ps[:], bias_rows_f32[:], ident[:])
-        bias_col = keep.tile([P, STACKS], F32)
-        nc.vector.tensor_copy(out=bias_col[:], in_=bias_ps[:, 0:STACKS])
+        def turn_h(t):
+            h_words = h_sb[t][:].bitcast(F32)
+            grouped = stage.tile([P, H], BF16, align_bytes=64)
+            grouped_words = grouped[:].bitcast(F32).rearrange("p (g b u) -> p g b u", g=PASSES, u=2)
+            for half in range(2):
+                turned_ps = psum.tile([P, 4, P], F32)
+                for g in range(2):
+                    for u in range(2):
+                        k_pass = 2 * half + g
+                        nc.tensor.transpose(
+                            turned_ps[:, 2 * g + u, :],
+                            h_words[:, WORDS * k_pass + u : WORDS * (k_pass + 1) : 2],
+                            ident[:],
+                        )
+                nc.scalar.copy(
+                    out=grouped_words[:, 2 * half : 2 * half + 2, :, :],
+                    in_=turned_ps[:].rearrange("p (g u) b -> p g b u", u=2),
+                )
+            return grouped
+
+        def multiply(grouped):
+            h_codes = stage.tile([P, PASSES * P], U32, align_bytes=64)
+            h_scales = stage.tile([P, PASSES * P], U8, align_bytes=64)
+            nc.vector.quantize_mx(out=h_codes[:].bitcast(FP8X4), scales=h_scales[:], in_=grouped[:])
+            push_t_ps = psum.tile([P, STACKS, P], F32)
+            for n in range(STACKS):
+                for g in range(PASSES):
+                    nc.tensor.matmul_mx(
+                        out=push_t_ps[:, n, :],
+                        lhsT=w_words[:, g, 2 * CELL * n : 2 * CELL * (n + 1)].bitcast(FP4X4),
+                        lhsT_scale=w_scales[:, g, CELL * n : CELL * (n + 1)],
+                        rhs=h_codes[:, P * g : P * (g + 1)].bitcast(FP8X4),
+                        rhs_scale=h_scales[:, P * g : P * (g + 1)],
+                        start=(g == 0),
+                        stop=(g == PASSES - 1),
+                    )
+            return push_t_ps
+
+        def add_bias_and_turn_back(push_t_ps):
+            push_t = stage.tile([P, STACKS, P], F32)
+            push_ps = psum.tile([P, STACKS, CELL], F32)
+            for n in range(STACKS):
+                nc.scalar.activation(
+                    out=push_t[:, n, :], in_=push_t_ps[:, n, :], func=ACT.Identity, bias=bias_col[:, n : n + 1], scale=1.0
+                )
+            for n in range(STACKS):
+                nc.tensor.transpose(push_ps[:, n, :], push_t[:, n, :], ident[:])
+            return push_ps
 
         def stay(t, acc, n):
             nc.scalar.activation(out=acc[:, n, :], in_=stack_sb[t][:, n, :], func=ACT.Copy, scale=weight(t, n, 2))
@@ -125,80 +167,41 @@ def tile_stackrnncore_pa_kernel(tc, h, act_logits, stacks, W_push_words, W_push_
                 op0=ALU.mult,
                 op1=ALU.add,
             )
+            nc.sync.dma_start(out=out_rows[:, t, n, CELL:DEPTH], in_=acc[:, n, CELL:DEPTH])
+
+        def push_on_top(t, acc, n, push_ps):
+            nc.vector.scalar_tensor_tensor(
+                out=acc[:, n, 0:CELL],
+                in0=push_ps[:, n, :],
+                scalar=weight(t, n, 0),
+                in1=acc[:, n, 0:CELL],
+                op0=ALU.mult,
+                op1=ALU.add,
+            )
+
+        bias_rows_f32 = keep.tile([P, P], F32)
+        nc.gpsimd.tensor_copy(out=bias_rows_f32[:], in_=bias_rows[:])
+        bias_ps = psum_once.tile([P, P], F32)
+        nc.tensor.transpose(bias_ps[:], bias_rows_f32[:], ident[:])
+        bias_col = keep.tile([P, STACKS], F32)
+        nc.vector.tensor_copy(out=bias_col[:], in_=bias_ps[:, 0:STACKS])
 
         for t in range(TILES):
             acc = blend.tile([P, STACKS, DEPTH], F32)
-
-            h_words = h_sb[t][:].bitcast(F32)
-            turned = []
-            for half in range(2):
-                turned_ps = psum.tile([P, 4, P], F32)
-                for g in range(2):
-                    for u in range(2):
-                        k_pass = 2 * half + g
-                        nc.tensor.transpose(
-                            turned_ps[:, 2 * g + u, :],
-                            h_words[:, WORDS * k_pass + u : WORDS * (k_pass + 1) : 2],
-                            ident[:],
-                        )
-                turned.append(turned_ps)
-
-            stay(t, acc, 0)
-            stay(t, acc, 1)
-            pop(t, acc, 0)
-            pop(t, acc, 1)
-
-            grouped = stage.tile([P, H], BF16, align_bytes=64)
-            grouped_words = grouped[:].bitcast(F32).rearrange("p (g b u) -> p g b u", g=PASSES, u=2)
-            for half in range(2):
-                nc.scalar.copy(
-                    out=grouped_words[:, 2 * half : 2 * half + 2, :, :],
-                    in_=turned[half][:].rearrange("p (g u) b -> p g b u", u=2),
-                )
-            h_codes = stage.tile([P, PASSES * P], U32, align_bytes=64)
-            h_scales = stage.tile([P, PASSES * P], U8, align_bytes=64)
-            nc.vector.quantize_mx(out=h_codes[:].bitcast(FP8X4), scales=h_scales[:], in_=grouped[:])
-
-            push_t_ps = psum.tile([P, STACKS, P], F32)
-            for n in range(STACKS):
-                for g in range(PASSES):
-                    nc.tensor.matmul_mx(
-                        out=push_t_ps[:, n, :],
-                        lhsT=w_words[:, g, 2 * CELL * n : 2 * CELL * (n + 1)].bitcast(FP4X4),
-                        lhsT_scale=w_scales[:, g, CELL * n : CELL * (n + 1)],
-                        rhs=h_codes[:, P * g : P * (g + 1)].bitcast(FP8X4),
-                        rhs_scale=h_scales[:, P * g : P * (g + 1)],
-                        start=(g == 0),
-                        stop=(g == PASSES - 1),
-                    )
-
-            shift_down(t, acc, 0)
-            shift_down(t, acc, 1)
-            nc.sync.dma_start(out=out_rows[:, t, 0:2, CELL:DEPTH], in_=acc[:, 0:2, CELL:DEPTH])
-
-            stay(t, acc, 2)
-            stay(t, acc, 3)
-            pop(t, acc, 2)
-            pop(t, acc, 3)
+            for n in (0, 1):
+                stay(t, acc, n)
+            for n in (0, 1):
+                pop(t, acc, n)
+            push_t_ps = multiply(turn_h(t))
+            for n in (0, 1):
+                shift_down(t, acc, n)
+            for n in (2, 3):
+                stay(t, acc, n)
+            for n in (2, 3):
+                pop(t, acc, n)
             shift_down(t, acc, 2)
-            shift_down(t, acc, 3)
-            nc.sync.dma_start(out=out_rows[:, t, 2:4, CELL:DEPTH], in_=acc[:, 2:4, CELL:DEPTH])
-
-            push_t = stage.tile([P, STACKS, P], F32)
-            push_ps = psum.tile([P, STACKS, CELL], F32)
+            push_ps = add_bias_and_turn_back(push_t_ps)
             for n in range(STACKS):
-                nc.scalar.activation(
-                    out=push_t[:, n, :], in_=push_t_ps[:, n, :], func=ACT.Identity, bias=bias_col[:, n : n + 1], scale=1.0
-                )
-            for n in range(STACKS):
-                nc.tensor.transpose(push_ps[:, n, :], push_t[:, n, :], ident[:])
-            for n in range(STACKS):
-                nc.vector.scalar_tensor_tensor(
-                    out=acc[:, n, 0:CELL],
-                    in0=push_ps[:, n, :],
-                    scalar=weight(t, n, 0),
-                    in1=acc[:, n, 0:CELL],
-                    op0=ALU.mult,
-                    op1=ALU.add,
-                )
+                push_on_top(t, acc, n, push_ps)
             nc.sync.dma_start(out=out_rows[:, t, :, 0:CELL], in_=acc[:, :, 0:CELL])
+            shift_down(t, acc, 3)

@@ -25,6 +25,9 @@ DEPTH = CELLS * CELL
 TILES = B // P
 PASSES = H // 512
 WORDS = 256
+BANK = 512
+SIDE_TILE = TILES - 1
+SIDE_STACKS = (2, 3)
 
 FLOPS = 2 * B * H * STACKS * CELL
 
@@ -40,7 +43,7 @@ def tile_stackrnncore_pa_kernel(tc, h, act_logits, stacks, W_push_words, W_push_
         stage = ctx.enter_context(tc.tile_pool(name="stage", bufs=2))
         blend = ctx.enter_context(tc.tile_pool(name="blend", bufs=4))
         psum = ctx.enter_context(tc.psum_pool(name="psum", bufs=2))
-        psum_once = ctx.enter_context(tc.psum_pool(name="psum_once", bufs=1))
+        psum_side = ctx.enter_context(tc.psum_pool(name="psum_side", bufs=2))
         ctx.enter_context(tc.manual_schedule())
 
         zero = keep.tile([P, 1], F32)
@@ -72,7 +75,12 @@ def tile_stackrnncore_pa_kernel(tc, h, act_logits, stacks, W_push_words, W_push_
         nc.sync.dma_start(out=stack_sb[0][:, 2:4, :], in_=stack_rows[:, 0, 2:4, :])
         for t in range(1, TILES):
             nc.sync.dma_start(out=h_sb[t][:], in_=h_rows[:, t, :])
-            nc.sync.dma_start(out=stack_sb[t][:], in_=stack_rows[:, t, :, :])
+            if t == SIDE_TILE:
+                nc.sync.dma_start(out=stack_sb[t][:, 0:2, :], in_=stack_rows[:, t, 0:2, :])
+            else:
+                nc.sync.dma_start(out=stack_sb[t][:], in_=stack_rows[:, t, :, :])
+            if t == 1:
+                nc.sync.dma_start(out=stack_sb[SIDE_TILE][:, 2:4, :], in_=stack_rows[:, SIDE_TILE, 2:4, :])
 
         shape = [P, TILES, STACKS * ACTIONS]
         top_logit = keep.tile([P, TILES], F32)
@@ -181,22 +189,64 @@ def tile_stackrnncore_pa_kernel(tc, h, act_logits, stacks, W_push_words, W_push_
 
         bias_rows_f32 = keep.tile([P, P], F32)
         nc.gpsimd.tensor_copy(out=bias_rows_f32[:], in_=bias_rows[:])
-        bias_ps = psum_once.tile([P, P], F32)
+        bias_ps = psum_side.tile([P, P], F32, tag="side")
         nc.tensor.transpose(bias_ps[:], bias_rows_f32[:], ident[:])
         bias_col = keep.tile([P, STACKS], F32)
         nc.vector.tensor_copy(out=bias_col[:], in_=bias_ps[:, 0:STACKS])
 
-        for t in range(TILES):
+        acc_side = keep.tile([P, STACKS, DEPTH], F32)
+        wide = {n: keep.tile([P, DEPTH], F32, name="wide%d" % n) for n in SIDE_STACKS}
+        diag = {}
+
+        def make_diagonals(n):
+            for action in range(ACTIONS):
+                diag[(n, action)] = keep.tile([P, P], F32, name="diag%d_%d" % (n, action))
+                nc.scalar.activation(
+                    out=diag[(n, action)][:], in_=ident[:], func=ACT.Copy, scale=weight(SIDE_TILE, n, action)
+                )
+
+        def widen(n, half):
+            columns = slice(0, 5 * CELL) if half == 0 else slice(5 * CELL, DEPTH)
+            nc.scalar.copy(out=wide[n][:, columns], in_=stack_sb[SIDE_TILE][:, n, columns])
+
+        def blend_on_tensor(n, half):
+            side_ps = psum_side.tile([P, BANK], F32, tag="side")
+            first = BANK * half
+            nc.tensor.matmul(side_ps[:], lhsT=diag[(n, 2)][:], rhs=wide[n][:, first : first + BANK], start=True, stop=False)
+            if half == 0:
+                nc.tensor.matmul(side_ps[:], lhsT=diag[(n, 1)][:], rhs=wide[n][:, CELL : CELL + BANK], start=False, stop=False)
+                nc.tensor.matmul(side_ps[:, CELL:BANK], lhsT=diag[(n, 0)][:], rhs=wide[n][:, 0 : BANK - CELL], start=False, stop=True)
+            else:
+                nc.tensor.matmul(side_ps[:], lhsT=diag[(n, 0)][:], rhs=wide[n][:, BANK - CELL : DEPTH - CELL], start=False, stop=False)
+                nc.tensor.matmul(side_ps[:, 0 : BANK - CELL], lhsT=diag[(n, 1)][:], rhs=wide[n][:, BANK + CELL : DEPTH], start=False, stop=True)
+            return side_ps
+
+        def empty_side(n, half, side_ps):
+            nc.scalar.copy(out=acc_side[:, n, BANK * half : BANK * (half + 1)], in_=side_ps[:])
+            if half == 1:
+                nc.sync.dma_start(out=out_rows[:, SIDE_TILE, n, CELL:DEPTH], in_=acc_side[:, n, CELL:DEPTH])
+
+        units = [(n, half) for n in SIDE_STACKS for half in (0, 1)]
+
+        for t in range(TILES - 1):
             acc = blend.tile([P, STACKS, DEPTH], F32)
             for n in (0, 1):
                 stay(t, acc, n)
             for n in (0, 1):
                 pop(t, acc, n)
-            push_t_ps = multiply(turn_h(t))
+            grouped = turn_h(t)
+            side_ps = blend_on_tensor(*units[t - 2]) if 2 <= t < 2 + len(units) else None
+            push_t_ps = multiply(grouped)
             for n in (0, 1):
                 shift_down(t, acc, n)
             for n in (2, 3):
                 stay(t, acc, n)
+            if t < len(SIDE_STACKS):
+                make_diagonals(SIDE_STACKS[t])
+            if side_ps is not None:
+                empty_side(*units[t - 2], side_ps)
+            if 1 <= t < 1 + len(units):
+                widen(*units[t - 1])
             for n in (2, 3):
                 pop(t, acc, n)
             shift_down(t, acc, 2)
@@ -205,3 +255,16 @@ def tile_stackrnncore_pa_kernel(tc, h, act_logits, stacks, W_push_words, W_push_
                 push_on_top(t, acc, n, push_ps)
             nc.sync.dma_start(out=out_rows[:, t, :, 0:CELL], in_=acc[:, :, 0:CELL])
             shift_down(t, acc, 3)
+
+        t = SIDE_TILE
+        push_t_ps = multiply(turn_h(t))
+        for n in (0, 1):
+            stay(t, acc_side, n)
+        for n in (0, 1):
+            pop(t, acc_side, n)
+        for n in (0, 1):
+            shift_down(t, acc_side, n)
+        push_ps = add_bias_and_turn_back(push_t_ps)
+        for n in range(STACKS):
+            push_on_top(t, acc_side, n, push_ps)
+        nc.sync.dma_start(out=out_rows[:, t, :, 0:CELL], in_=acc_side[:, :, 0:CELL])

@@ -156,6 +156,11 @@ def tile_stackrnncore_pa_kernel(tc, h, act_logits, stacks, W_push_words, W_push_
         def stay(t, acc, n):
             nc.scalar.activation(out=acc[:, n, :], in_=stack_sb[t][:, n, :], func=ACT.Copy, scale=weight(t, n, 2))
 
+        def stay_on_vector(t, acc, n):
+            nc.vector.tensor_scalar(
+                out=acc[:, n, :], in0=stack_sb[t][:, n, :], scalar1=weight(t, n, 2), scalar2=None, op0=ALU.mult
+            )
+
         def pop(t, acc, n):
             nc.vector.scalar_tensor_tensor(
                 out=acc[:, n, 0 : DEPTH - CELL],
@@ -230,8 +235,11 @@ def tile_stackrnncore_pa_kernel(tc, h, act_logits, stacks, W_push_words, W_push_
 
         for t in range(TILES - 1):
             acc = blend.tile([P, STACKS, DEPTH], F32)
-            for n in (0, 1):
-                stay(t, acc, n)
+            if t == 0:
+                stay_on_vector(t, acc, 0)
+            else:
+                stay(t, acc, 0)
+            stay(t, acc, 1)
             for n in (0, 1):
                 pop(t, acc, n)
             grouped = turn_h(t)

@@ -28,6 +28,8 @@ WORDS = 256
 BANK = 512
 SIDE_TILE = TILES - 1
 SIDE_STACKS = (2, 3)
+PART_STACK = 1
+PART_FIRST = 6
 
 FLOPS = 2 * B * H * STACKS * CELL
 
@@ -62,7 +64,8 @@ def tile_stackrnncore_pa_kernel(tc, h, act_logits, stacks, W_push_words, W_push_
         stack_sb = [keep.tile([P, STACKS, DEPTH], BF16, name="stack_sb%d" % t) for t in range(TILES)]
         h_sb = [keep.tile([P, H], BF16, name="h_sb%d" % t) for t in range(TILES)]
         w_words = keep.tile([P, PASSES, 2 * STACKS * CELL], U8, align_bytes=64)
-        nc.sync.dma_start(out=stack_sb[0][:, 0:2, :], in_=stack_rows[:, 0, 0:2, :])
+        nc.sync.dma_start(out=stack_sb[0][:, 0, :], in_=stack_rows[:, 0, 0, :])
+        nc.sync.dma_start(out=stack_sb[0][:, 1, :], in_=stack_rows[:, 0, 1, :])
         nc.sync.dma_start(out=bias_rows[0:STACKS, :], in_=b_push.rearrange("(n c) -> n c", n=STACKS))
         nc.sync.dma_start(out=h_sb[0][:], in_=h_rows[:, 0, :])
         scale_words = W_push_scales.bitcast(I32)
@@ -83,22 +86,39 @@ def tile_stackrnncore_pa_kernel(tc, h, act_logits, stacks, W_push_words, W_push_
                 nc.sync.dma_start(out=stack_sb[SIDE_TILE][:, 2:4, :], in_=stack_rows[:, SIDE_TILE, 2:4, :])
 
         shape = [P, TILES, STACKS * ACTIONS]
-        top_logit = keep.tile([P, TILES], F32)
-        nc.vector.tensor_reduce(out=top_logit[:], in_=logits[:], axis=AXIS_X, op=ALU.max)
-        shifted = keep.tile(shape, F32)
-        nc.vector.tensor_tensor(
-            out=shifted[:], in0=logits[:], in1=top_logit[:].unsqueeze(2).to_broadcast(shape), op=ALU.subtract
-        )
+        minus_top = keep.tile([P, TILES], F32)
+        nc.vector.tensor_reduce(out=minus_top[:], in_=logits[:], axis=AXIS_X, op=ALU.max, negate=True)
         expd = keep.tile(shape, F32)
-        nc.scalar.activation(out=expd[:], in_=shifted[:], func=ACT.Exp)
         total = keep.tile([P, TILES], F32)
-        nc.vector.tensor_reduce(out=total[:], in_=expd[:], axis=AXIS_X, op=ALU.add)
         inverse = keep.tile([P, TILES], F32)
-        nc.vector.reciprocal(out=inverse[:], in_=total[:])
         weights = keep.tile(shape, F32)
-        nc.vector.tensor_tensor(
-            out=weights[:], in0=expd[:], in1=inverse[:].unsqueeze(2).to_broadcast(shape), op=ALU.mult
-        )
+
+        def exponentials(tiles):
+            for t in tiles:
+                nc.scalar.activation(
+                    out=expd[:, t, :],
+                    in_=logits[:, t, :],
+                    func=ACT.Exp,
+                    bias=minus_top[:, t : t + 1],
+                    scale=1.0,
+                    accum_out=total[:, t : t + 1],
+                )
+
+        def invert_totals(tiles):
+            nc.vector.reciprocal(out=inverse[:, tiles], in_=total[:, tiles])
+
+        def normalise(tiles):
+            nc.vector.tensor_tensor(
+                out=weights[:, tiles, :],
+                in0=expd[:, tiles, :],
+                in1=inverse[:, tiles].unsqueeze(2).to_broadcast([P, tiles.stop - tiles.start, STACKS * ACTIONS]),
+                op=ALU.mult,
+            )
+
+        first_tile = slice(0, 1)
+        other_tiles = slice(1, TILES)
+        exponentials(range(0, 1))
+        invert_totals(first_tile)
 
         def weight(t, n, action):
             column = ACTIONS * n + action
@@ -153,34 +173,45 @@ def tile_stackrnncore_pa_kernel(tc, h, act_logits, stacks, W_push_words, W_push_
                 nc.tensor.transpose(push_ps[:, n, :], push_t[:, n, :], ident[:])
             return push_ps
 
-        def stay(t, acc, n):
-            nc.scalar.activation(out=acc[:, n, :], in_=stack_sb[t][:, n, :], func=ACT.Copy, scale=weight(t, n, 2))
+        def stay(t, acc, n, cells=CELLS):
+            width = CELL * cells
+            nc.scalar.activation(
+                out=acc[:, n, 0:width], in_=stack_sb[t][:, n, 0:width], func=ACT.Copy, scale=weight(t, n, 2)
+            )
 
         def stay_on_vector(t, acc, n):
+            column = ACTIONS * n + 2
             nc.vector.tensor_scalar(
-                out=acc[:, n, :], in0=stack_sb[t][:, n, :], scalar1=weight(t, n, 2), scalar2=None, op0=ALU.mult
+                out=acc[:, n, :],
+                in0=stack_sb[t][:, n, :],
+                scalar1=expd[:, t, column : column + 1],
+                scalar2=inverse[:, t : t + 1],
+                op0=ALU.mult,
+                op1=ALU.mult,
             )
 
-        def pop(t, acc, n):
+        def pop(t, acc, n, cells=CELLS):
+            width = CELL * min(cells, CELLS - 1)
             nc.vector.scalar_tensor_tensor(
-                out=acc[:, n, 0 : DEPTH - CELL],
-                in0=stack_sb[t][:, n, CELL:DEPTH],
+                out=acc[:, n, 0:width],
+                in0=stack_sb[t][:, n, CELL : CELL + width],
                 scalar=weight(t, n, 1),
-                in1=acc[:, n, 0 : DEPTH - CELL],
+                in1=acc[:, n, 0:width],
                 op0=ALU.mult,
                 op1=ALU.add,
             )
 
-        def shift_down(t, acc, n):
+        def shift_down(t, acc, n, cells=CELLS):
+            width = CELL * cells
             nc.vector.scalar_tensor_tensor(
-                out=acc[:, n, CELL:DEPTH],
-                in0=stack_sb[t][:, n, 0 : DEPTH - CELL],
+                out=acc[:, n, CELL:width],
+                in0=stack_sb[t][:, n, 0 : width - CELL],
                 scalar=weight(t, n, 0),
-                in1=acc[:, n, CELL:DEPTH],
+                in1=acc[:, n, CELL:width],
                 op0=ALU.mult,
                 op1=ALU.add,
             )
-            nc.sync.dma_start(out=out_rows[:, t, n, CELL:DEPTH], in_=acc[:, n, CELL:DEPTH])
+            nc.sync.dma_start(out=out_rows[:, t, n, CELL:width], in_=acc[:, n, CELL:width])
 
         def push_on_top(t, acc, n, push_ps):
             nc.vector.scalar_tensor_tensor(
@@ -197,10 +228,9 @@ def tile_stackrnncore_pa_kernel(tc, h, act_logits, stacks, W_push_words, W_push_
         bias_ps = psum_side.tile([P, P], F32, tag="side")
         nc.tensor.transpose(bias_ps[:], bias_rows_f32[:], ident[:])
         bias_col = keep.tile([P, STACKS], F32)
-        nc.vector.tensor_copy(out=bias_col[:], in_=bias_ps[:, 0:STACKS])
 
         acc_side = keep.tile([P, STACKS, DEPTH], F32)
-        wide = {n: keep.tile([P, DEPTH], F32, name="wide%d" % n) for n in SIDE_STACKS}
+        wide = {n: keep.tile([P, DEPTH], F32, name="wide%d" % n) for n in SIDE_STACKS + (PART_STACK,)}
         diag = {}
 
         def make_diagonals(n):
@@ -231,48 +261,90 @@ def tile_stackrnncore_pa_kernel(tc, h, act_logits, stacks, W_push_words, W_push_
             if half == 1:
                 nc.sync.dma_start(out=out_rows[:, SIDE_TILE, n, CELL:DEPTH], in_=acc_side[:, n, CELL:DEPTH])
 
+        def widen_part():
+            columns = slice(CELL * (PART_FIRST - 1), DEPTH)
+            nc.scalar.copy(out=wide[PART_STACK][:, columns], in_=stack_sb[SIDE_TILE][:, PART_STACK, columns])
+
+        def blend_part_on_tensor():
+            n = PART_STACK
+            first = CELL * PART_FIRST
+            width = DEPTH - first
+            part_ps = psum_side.tile([P, BANK], F32, tag="side")
+            nc.tensor.matmul(part_ps[:, 0:width], lhsT=diag[(n, 2)][:], rhs=wide[n][:, first:DEPTH], start=True, stop=False)
+            nc.tensor.matmul(part_ps[:, 0:width], lhsT=diag[(n, 0)][:], rhs=wide[n][:, first - CELL : DEPTH - CELL], start=False, stop=False)
+            nc.tensor.matmul(part_ps[:, 0 : width - CELL], lhsT=diag[(n, 1)][:], rhs=wide[n][:, first + CELL : DEPTH], start=False, stop=True)
+            return part_ps
+
+        def empty_part(part_ps):
+            first = CELL * PART_FIRST
+            nc.scalar.copy(out=acc_side[:, PART_STACK, first:DEPTH], in_=part_ps[:, 0 : DEPTH - first])
+            nc.sync.dma_start(out=out_rows[:, SIDE_TILE, PART_STACK, first:DEPTH], in_=acc_side[:, PART_STACK, first:DEPTH])
+
         units = [(n, half) for n in SIDE_STACKS for half in (0, 1)]
 
         for t in range(TILES - 1):
             acc = blend.tile([P, STACKS, DEPTH], F32)
             if t == 0:
                 stay_on_vector(t, acc, 0)
+                normalise(first_tile)
+                stay_on_vector(t, acc, 1)
+                nc.vector.tensor_copy(out=bias_col[:], in_=bias_ps[:, 0:STACKS])
+                for n in (0, 1):
+                    pop(t, acc, n)
+                grouped = turn_h(t)
+                exponentials(range(1, TILES))
+                shift_down(t, acc, 0)
+                push_t_ps = multiply(grouped)
+                invert_totals(other_tiles)
+                shift_down(t, acc, 1)
+                normalise(other_tiles)
             else:
-                stay(t, acc, 0)
-            stay(t, acc, 1)
-            for n in (0, 1):
-                pop(t, acc, n)
-            grouped = turn_h(t)
-            side_ps = blend_on_tensor(*units[t - 2]) if 2 <= t < 2 + len(units) else None
-            push_t_ps = multiply(grouped)
-            for n in (0, 1):
-                shift_down(t, acc, n)
+                for n in (0, 1):
+                    stay(t, acc, n)
+                for n in (0, 1):
+                    pop(t, acc, n)
+                grouped = turn_h(t)
+                side_ps = blend_on_tensor(*units[t - 2]) if 2 <= t < 2 + len(units) else None
+                part_ps = blend_part_on_tensor() if t == 2 + len(units) else None
+                push_t_ps = multiply(grouped)
+                for n in (0, 1):
+                    shift_down(t, acc, n)
             for n in (2, 3):
                 stay(t, acc, n)
             if t < len(SIDE_STACKS):
                 make_diagonals(SIDE_STACKS[t])
-            if side_ps is not None:
+            if 2 <= t < 2 + len(units):
                 empty_side(*units[t - 2], side_ps)
             if 1 <= t < 1 + len(units):
                 widen(*units[t - 1])
+            if t == 1 + len(units):
+                make_diagonals(PART_STACK)
+                widen_part()
+            if t == 2 + len(units):
+                empty_part(part_ps)
+            if t == SIDE_TILE - 1:
+                last_grouped = turn_h(SIDE_TILE)
             for n in (2, 3):
                 pop(t, acc, n)
             shift_down(t, acc, 2)
             push_ps = add_bias_and_turn_back(push_t_ps)
+            if t == SIDE_TILE - 1:
+                last_push_t_ps = multiply(last_grouped)
             for n in range(STACKS):
                 push_on_top(t, acc, n, push_ps)
             nc.sync.dma_start(out=out_rows[:, t, :, 0:CELL], in_=acc[:, :, 0:CELL])
+            if t == SIDE_TILE - 1:
+                stay(SIDE_TILE, acc_side, 0)
+                pop(SIDE_TILE, acc_side, 0)
             shift_down(t, acc, 3)
 
         t = SIDE_TILE
-        push_t_ps = multiply(turn_h(t))
-        for n in (0, 1):
-            stay(t, acc_side, n)
-        for n in (0, 1):
-            pop(t, acc_side, n)
-        for n in (0, 1):
-            shift_down(t, acc_side, n)
-        push_ps = add_bias_and_turn_back(push_t_ps)
-        for n in range(STACKS):
+        mine = {0: CELLS, PART_STACK: PART_FIRST}
+        stay(t, acc_side, 1, mine[1])
+        push_ps = add_bias_and_turn_back(last_push_t_ps)
+        shift_down(t, acc_side, 0, mine[0])
+        pop(t, acc_side, 1, mine[1])
+        for n in (2, 3, 0, 1):
             push_on_top(t, acc_side, n, push_ps)
         nc.sync.dma_start(out=out_rows[:, t, :, 0:CELL], in_=acc_side[:, :, 0:CELL])
+        shift_down(t, acc_side, 1, mine[1])

@@ -66,8 +66,8 @@ def tile_stackrnncore_pa_kernel(tc, h, act_logits, stacks, W_push_words, W_push_
         w_words = keep.tile([P, PASSES, 2 * STACKS * CELL], U8, align_bytes=64)
         nc.sync.dma_start(out=stack_sb[0][:, 0, :], in_=stack_rows[:, 0, 0, :])
         nc.sync.dma_start(out=stack_sb[0][:, 1, :], in_=stack_rows[:, 0, 1, :])
-        nc.sync.dma_start(out=bias_rows[0:STACKS, :], in_=b_push.rearrange("(n c) -> n c", n=STACKS))
         nc.sync.dma_start(out=h_sb[0][:], in_=h_rows[:, 0, :])
+        nc.sync.dma_start(out=stack_sb[0][:, 2:4, :], in_=stack_rows[:, 0, 2:4, :])
         scale_words = W_push_scales.bitcast(I32)
         for quad in range(4):
             nc.sync.dma_start(
@@ -75,7 +75,7 @@ def tile_stackrnncore_pa_kernel(tc, h, act_logits, stacks, W_push_words, W_push_
                 in_=scale_words[:, 4 * quad : 4 * quad + 4, :].rearrange("g r w -> r g w"),
             )
         nc.sync.dma_start(out=w_words[:].bitcast(I32), in_=W_push_words.bitcast(I32).rearrange("g p w -> p g w"))
-        nc.sync.dma_start(out=stack_sb[0][:, 2:4, :], in_=stack_rows[:, 0, 2:4, :])
+        nc.sync.dma_start(out=bias_rows[0:STACKS, :], in_=b_push.rearrange("(n c) -> n c", n=STACKS))
         for t in range(1, TILES):
             nc.sync.dma_start(out=h_sb[t][:], in_=h_rows[:, t, :])
             if t == SIDE_TILE:
@@ -201,17 +201,18 @@ def tile_stackrnncore_pa_kernel(tc, h, act_logits, stacks, W_push_words, W_push_
                 op1=ALU.add,
             )
 
-        def shift_down(t, acc, n, cells=CELLS):
+        def shift_down(t, acc, n, cells=CELLS, first=1):
+            low = CELL * first
             width = CELL * cells
             nc.vector.scalar_tensor_tensor(
-                out=acc[:, n, CELL:width],
-                in0=stack_sb[t][:, n, 0 : width - CELL],
+                out=acc[:, n, low:width],
+                in0=stack_sb[t][:, n, low - CELL : width - CELL],
                 scalar=weight(t, n, 0),
-                in1=acc[:, n, CELL:width],
+                in1=acc[:, n, low:width],
                 op0=ALU.mult,
                 op1=ALU.add,
             )
-            nc.sync.dma_start(out=out_rows[:, t, n, CELL:width], in_=acc[:, n, CELL:width])
+            nc.sync.dma_start(out=out_rows[:, t, n, low:width], in_=acc[:, n, low:width])
 
         def push_on_top(t, acc, n, push_ps):
             nc.vector.scalar_tensor_tensor(
@@ -223,11 +224,14 @@ def tile_stackrnncore_pa_kernel(tc, h, act_logits, stacks, W_push_words, W_push_
                 op1=ALU.add,
             )
 
-        bias_rows_f32 = keep.tile([P, P], F32)
-        nc.gpsimd.tensor_copy(out=bias_rows_f32[:], in_=bias_rows[:])
-        bias_ps = psum_side.tile([P, P], F32, tag="side")
-        nc.tensor.transpose(bias_ps[:], bias_rows_f32[:], ident[:])
         bias_col = keep.tile([P, STACKS], F32)
+
+        def turn_bias():
+            bias_rows_f32 = keep.tile([P, P], F32)
+            nc.scalar.copy(out=bias_rows_f32[:], in_=bias_rows[:])
+            bias_ps = psum_side.tile([P, P], F32, tag="side")
+            nc.tensor.transpose(bias_ps[:], bias_rows_f32[:], ident[:])
+            return bias_ps
 
         acc_side = keep.tile([P, STACKS, DEPTH], F32)
         wide = {n: keep.tile([P, DEPTH], F32, name="wide%d" % n) for n in SIDE_STACKS + (PART_STACK,)}
@@ -288,11 +292,11 @@ def tile_stackrnncore_pa_kernel(tc, h, act_logits, stacks, W_push_words, W_push_
                 stay_on_vector(t, acc, 0)
                 normalise(first_tile)
                 stay_on_vector(t, acc, 1)
-                nc.vector.tensor_copy(out=bias_col[:], in_=bias_ps[:, 0:STACKS])
                 for n in (0, 1):
                     pop(t, acc, n)
                 grouped = turn_h(t)
                 exponentials(range(1, TILES))
+                bias_ps = turn_bias()
                 shift_down(t, acc, 0)
                 push_t_ps = multiply(grouped)
                 invert_totals(other_tiles)
@@ -311,6 +315,8 @@ def tile_stackrnncore_pa_kernel(tc, h, act_logits, stacks, W_push_words, W_push_
                     shift_down(t, acc, n)
             for n in (2, 3):
                 stay(t, acc, n)
+            if t == 0:
+                nc.scalar.copy(out=bias_col[:], in_=bias_ps[:, 0:STACKS])
             if t < len(SIDE_STACKS):
                 make_diagonals(SIDE_STACKS[t])
             if 2 <= t < 2 + len(units):
@@ -347,4 +353,5 @@ def tile_stackrnncore_pa_kernel(tc, h, act_logits, stacks, W_push_words, W_push_
         for n in (2, 3, 0, 1):
             push_on_top(t, acc_side, n, push_ps)
         nc.sync.dma_start(out=out_rows[:, t, :, 0:CELL], in_=acc_side[:, :, 0:CELL])
-        shift_down(t, acc_side, 1, mine[1])
+        shift_down(t, acc_side, 1, 4)
+        shift_down(t, acc_side, 1, mine[1], 4)

@@ -124,10 +124,9 @@ def tile_stackrnncore_pa_kernel(tc, h, act_logits, stacks, W_push_words, W_push_
             column = ACTIONS * n + action
             return weights[:, t, column : column + 1]
 
-        def turn_h(t):
+        def transpose_h(t):
             h_words = h_sb[t][:].bitcast(F32)
-            grouped = stage.tile([P, H], BF16, align_bytes=64)
-            grouped_words = grouped[:].bitcast(F32).rearrange("p (g b u) -> p g b u", g=PASSES, u=2)
+            turned = []
             for half in range(2):
                 turned_ps = psum.tile([P, 4, P], F32)
                 for g in range(2):
@@ -138,9 +137,16 @@ def tile_stackrnncore_pa_kernel(tc, h, act_logits, stacks, W_push_words, W_push_
                             h_words[:, WORDS * k_pass + u : WORDS * (k_pass + 1) : 2],
                             ident[:],
                         )
+                turned.append(turned_ps)
+            return turned
+
+        def copy_h(turned):
+            grouped = stage.tile([P, H], BF16, align_bytes=64)
+            grouped_words = grouped[:].bitcast(F32).rearrange("p (g b u) -> p g b u", g=PASSES, u=2)
+            for half in range(2):
                 nc.scalar.copy(
                     out=grouped_words[:, 2 * half : 2 * half + 2, :, :],
-                    in_=turned_ps[:].rearrange("p (g u) b -> p g b u", u=2),
+                    in_=turned[half][:].rearrange("p (g u) b -> p g b u", u=2),
                 )
             return grouped
 
@@ -286,7 +292,14 @@ def tile_stackrnncore_pa_kernel(tc, h, act_logits, stacks, W_push_words, W_push_
 
         units = [(n, half) for n in SIDE_STACKS for half in (0, 1)]
 
+        def finish_tops(t, acc, push_ps, order):
+            for n in order:
+                push_on_top(t, acc, n, push_ps)
+            nc.sync.dma_start(out=out_rows[:, t, :, 0:CELL], in_=acc[:, :, 0:CELL])
+
         for t in range(TILES - 1):
+            if t > 0:
+                before, before_push_t_ps = acc, push_t_ps
             acc = blend.tile([P, STACKS, DEPTH], F32)
             if t == 0:
                 stay_on_vector(t, acc, 0)
@@ -294,25 +307,29 @@ def tile_stackrnncore_pa_kernel(tc, h, act_logits, stacks, W_push_words, W_push_
                 stay_on_vector(t, acc, 1)
                 for n in (0, 1):
                     pop(t, acc, n)
-                grouped = turn_h(t)
+                grouped = copy_h(transpose_h(t))
                 exponentials(range(1, TILES))
                 bias_ps = turn_bias()
                 shift_down(t, acc, 0)
                 push_t_ps = multiply(grouped)
+                turned = transpose_h(t + 1)
                 invert_totals(other_tiles)
                 shift_down(t, acc, 1)
                 normalise(other_tiles)
             else:
                 for n in (0, 1):
                     stay(t, acc, n)
+                push_ps = add_bias_and_turn_back(before_push_t_ps)
                 for n in (0, 1):
                     pop(t, acc, n)
-                grouped = turn_h(t)
+                grouped = copy_h(turned)
                 side_ps = blend_on_tensor(*units[t - 2]) if 2 <= t < 2 + len(units) else None
                 part_ps = blend_part_on_tensor() if t == 2 + len(units) else None
                 push_t_ps = multiply(grouped)
+                turned = transpose_h(t + 1)
                 for n in (0, 1):
                     shift_down(t, acc, n)
+                finish_tops(t - 1, before, push_ps, range(STACKS))
             for n in (2, 3):
                 stay(t, acc, n)
             if t == 0:
@@ -329,17 +346,12 @@ def tile_stackrnncore_pa_kernel(tc, h, act_logits, stacks, W_push_words, W_push_
             if t == 2 + len(units):
                 empty_part(part_ps)
             if t == SIDE_TILE - 1:
-                last_grouped = turn_h(SIDE_TILE)
+                last_grouped = copy_h(turned)
             for n in (2, 3):
                 pop(t, acc, n)
             shift_down(t, acc, 2)
-            push_ps = add_bias_and_turn_back(push_t_ps)
             if t == SIDE_TILE - 1:
                 last_push_t_ps = multiply(last_grouped)
-            for n in range(STACKS):
-                push_on_top(t, acc, n, push_ps)
-            nc.sync.dma_start(out=out_rows[:, t, :, 0:CELL], in_=acc[:, :, 0:CELL])
-            if t == SIDE_TILE - 1:
                 stay(SIDE_TILE, acc_side, 0)
                 pop(SIDE_TILE, acc_side, 0)
             shift_down(t, acc, 3)
@@ -347,11 +359,11 @@ def tile_stackrnncore_pa_kernel(tc, h, act_logits, stacks, W_push_words, W_push_
         t = SIDE_TILE
         mine = {0: CELLS, PART_STACK: PART_FIRST}
         stay(t, acc_side, 1, mine[1])
-        push_ps = add_bias_and_turn_back(last_push_t_ps)
+        push_ps = add_bias_and_turn_back(push_t_ps)
+        last_push_ps = add_bias_and_turn_back(last_push_t_ps)
         shift_down(t, acc_side, 0, mine[0])
         pop(t, acc_side, 1, mine[1])
-        for n in (2, 3, 0, 1):
-            push_on_top(t, acc_side, n, push_ps)
-        nc.sync.dma_start(out=out_rows[:, t, :, 0:CELL], in_=acc_side[:, :, 0:CELL])
+        finish_tops(t - 1, acc, push_ps, range(STACKS))
+        finish_tops(t, acc_side, last_push_ps, (2, 3, 0, 1))
         shift_down(t, acc_side, 1, 4)
         shift_down(t, acc_side, 1, mine[1], 4)

@@ -351,6 +351,7 @@ def tile_stackrnncore_pa_kernel(tc, h, act_logits, stacks, W_push_words, W_push_
                 pop(t, acc, n)
             shift_down(t, acc, 2)
             if t == SIDE_TILE - 1:
+                push_ps = add_bias_and_turn_back(push_t_ps)
                 last_push_t_ps = multiply(last_grouped)
                 stay(SIDE_TILE, acc_side, 0)
                 pop(SIDE_TILE, acc_side, 0)
@@ -358,12 +359,11 @@ def tile_stackrnncore_pa_kernel(tc, h, act_logits, stacks, W_push_words, W_push_
 
         t = SIDE_TILE
         mine = {0: CELLS, PART_STACK: PART_FIRST}
+        finish_tops(t - 1, acc, push_ps, range(STACKS))
         stay(t, acc_side, 1, mine[1])
-        push_ps = add_bias_and_turn_back(push_t_ps)
         last_push_ps = add_bias_and_turn_back(last_push_t_ps)
         shift_down(t, acc_side, 0, mine[0])
         pop(t, acc_side, 1, mine[1])
-        finish_tops(t - 1, acc, push_ps, range(STACKS))
         finish_tops(t, acc_side, last_push_ps, (2, 3, 0, 1))
         shift_down(t, acc_side, 1, 4)
         shift_down(t, acc_side, 1, mine[1], 4)

@@ -30,6 +30,7 @@ SIDE_TILE = TILES - 1
 SIDE_STACKS = (2, 3)
 PART_STACK = 1
 PART_FIRST = 6
+AHEAD = 4
 
 FLOPS = 2 * B * H * STACKS * CELL
 
@@ -76,14 +77,18 @@ def tile_stackrnncore_pa_kernel(tc, h, act_logits, stacks, W_push_words, W_push_
             )
         nc.sync.dma_start(out=w_words[:].bitcast(I32), in_=W_push_words.bitcast(I32).rearrange("g p w -> p g w"))
         nc.sync.dma_start(out=bias_rows[0:STACKS, :], in_=b_push.rearrange("(n c) -> n c", n=STACKS))
-        for t in range(1, TILES):
+
+        def load_tile(t):
             nc.sync.dma_start(out=h_sb[t][:], in_=h_rows[:, t, :])
             if t == SIDE_TILE:
                 nc.sync.dma_start(out=stack_sb[t][:, 0:2, :], in_=stack_rows[:, t, 0:2, :])
             else:
                 nc.sync.dma_start(out=stack_sb[t][:], in_=stack_rows[:, t, :, :])
-            if t == 1:
-                nc.sync.dma_start(out=stack_sb[SIDE_TILE][:, 2:4, :], in_=stack_rows[:, SIDE_TILE, 2:4, :])
+
+        load_tile(1)
+        nc.sync.dma_start(out=stack_sb[SIDE_TILE][:, 2:4, :], in_=stack_rows[:, SIDE_TILE, 2:4, :])
+        for t in range(2, AHEAD):
+            load_tile(t)
 
         shape = [P, TILES, STACKS * ACTIONS]
         minus_top = keep.tile([P, TILES], F32)
@@ -330,6 +335,8 @@ def tile_stackrnncore_pa_kernel(tc, h, act_logits, stacks, W_push_words, W_push_
                 for n in (0, 1):
                     shift_down(t, acc, n)
                 finish_tops(t - 1, before, push_ps, range(STACKS))
+            if t + AHEAD < TILES:
+                load_tile(t + AHEAD)
             for n in (2, 3):
                 stay(t, acc, n)
             if t == 0:

@@ -30,7 +30,7 @@ SIDE_TILE = TILES - 1
 SIDE_STACKS = (2, 3)
 PART_STACK = 1
 PART_FIRST = 6
-AHEAD = 4
+AHEAD = 3
 
 FLOPS = 2 * B * H * STACKS * CELL
 

@@ -53,10 +53,10 @@ def tile_stackrnncore_pa_kernel(tc, h, act_logits, stacks, W_push_words, W_push_
         nc.gpsimd.memset(zero[:], 0.0)
         one = keep.tile([P, 1], F32)
         nc.scalar.activation(out=one[:], in_=zero[:], func=ACT.Exp)
-        ident = keep.tile([P, P], F32)
-        make_identity(nc, ident[:])
         bias_rows = keep.tile([P, P], BF16)
         nc.gpsimd.memset(bias_rows[:], 0.0)
+        ident = keep.tile([P, P], F32)
+        make_identity(nc, ident[:])
         w_scales = keep.tile([P, PASSES, STACKS * CELL], U8, align_bytes=64)
         nc.vector.memset(w_scales[:].bitcast(I32), 0)
 
@@ -65,30 +65,34 @@ def tile_stackrnncore_pa_kernel(tc, h, act_logits, stacks, W_push_words, W_push_
         stack_sb = [keep.tile([P, STACKS, DEPTH], BF16, name="stack_sb%d" % t) for t in range(TILES)]
         h_sb = [keep.tile([P, H], BF16, name="h_sb%d" % t) for t in range(TILES)]
         w_words = keep.tile([P, PASSES, 2 * STACKS * CELL], U8, align_bytes=64)
-        nc.sync.dma_start(out=stack_sb[0][:, 0, :], in_=stack_rows[:, 0, 0, :])
-        nc.sync.dma_start(out=stack_sb[0][:, 1, :], in_=stack_rows[:, 0, 1, :])
-        nc.sync.dma_start(out=h_sb[0][:], in_=h_rows[:, 0, :])
-        nc.sync.dma_start(out=stack_sb[0][:, 2:4, :], in_=stack_rows[:, 0, 2:4, :])
         scale_words = W_push_scales.bitcast(I32)
-        for quad in range(4):
-            nc.sync.dma_start(
-                out=w_scales[32 * quad : 32 * quad + 4, :, :].bitcast(I32),
-                in_=scale_words[:, 4 * quad : 4 * quad + 4, :].rearrange("g r w -> r g w"),
-            )
-        nc.sync.dma_start(out=w_words[:].bitcast(I32), in_=W_push_words.bitcast(I32).rearrange("g p w -> p g w"))
-        nc.sync.dma_start(out=bias_rows[0:STACKS, :], in_=b_push.rearrange("(n c) -> n c", n=STACKS))
 
-        def load_tile(t):
+        def load_h(t):
             nc.sync.dma_start(out=h_sb[t][:], in_=h_rows[:, t, :])
-            if t == SIDE_TILE:
-                nc.sync.dma_start(out=stack_sb[t][:, 0:2, :], in_=stack_rows[:, t, 0:2, :])
-            else:
-                nc.sync.dma_start(out=stack_sb[t][:], in_=stack_rows[:, t, :, :])
 
-        load_tile(1)
-        nc.sync.dma_start(out=stack_sb[SIDE_TILE][:, 2:4, :], in_=stack_rows[:, SIDE_TILE, 2:4, :])
-        for t in range(2, AHEAD):
-            load_tile(t)
+        def load_stacks(t, first=0, end=STACKS):
+            nc.sync.dma_start(out=stack_sb[t][:, first:end, :], in_=stack_rows[:, t, first:end, :])
+
+        def load_weight():
+            for quad in range(4):
+                nc.sync.dma_start(
+                    out=w_scales[32 * quad : 32 * quad + 4, :, :].bitcast(I32),
+                    in_=scale_words[:, 4 * quad : 4 * quad + 4, :].rearrange("g r w -> r g w"),
+                )
+            nc.sync.dma_start(out=w_words[:].bitcast(I32), in_=W_push_words.bitcast(I32).rearrange("g p w -> p g w"))
+            nc.sync.dma_start(out=bias_rows[0:STACKS, :], in_=b_push.rearrange("(n c) -> n c", n=STACKS))
+
+        load_stacks(0, 0, 1)
+        load_stacks(0, 1, 2)
+        load_h(0)
+        load_stacks(0, 2, 4)
+        load_stacks(1, 0, 2)
+        load_weight()
+        load_h(1)
+        load_stacks(1, 2, 4)
+        load_h(2)
+        load_stacks(2)
+        load_stacks(SIDE_TILE, 2, 4)
 
         shape = [P, TILES, STACKS * ACTIONS]
         minus_top = keep.tile([P, TILES], F32)
@@ -314,20 +318,24 @@ def tile_stackrnncore_pa_kernel(tc, h, act_logits, stacks, W_push_words, W_push_
                     pop(t, acc, n)
                 grouped = copy_h(transpose_h(t))
                 exponentials(range(1, TILES))
-                bias_ps = turn_bias()
                 shift_down(t, acc, 0)
                 push_t_ps = multiply(grouped)
-                turned = transpose_h(t + 1)
+                turned = transpose_h(1)
                 invert_totals(other_tiles)
                 shift_down(t, acc, 1)
                 normalise(other_tiles)
             else:
                 for n in (0, 1):
                     stay(t, acc, n)
+                if t == 1:
+                    grouped = copy_h(turned)
+                    bias_ps = turn_bias()
+                    nc.scalar.copy(out=bias_col[:], in_=bias_ps[:, 0:STACKS])
                 push_ps = add_bias_and_turn_back(before_push_t_ps)
                 for n in (0, 1):
                     pop(t, acc, n)
-                grouped = copy_h(turned)
+                if t > 1:
+                    grouped = copy_h(turned)
                 side_ps = blend_on_tensor(*units[t - 2]) if 2 <= t < 2 + len(units) else None
                 part_ps = blend_part_on_tensor() if t == 2 + len(units) else None
                 push_t_ps = multiply(grouped)
@@ -336,13 +344,14 @@ def tile_stackrnncore_pa_kernel(tc, h, act_logits, stacks, W_push_words, W_push_
                     shift_down(t, acc, n)
                 finish_tops(t - 1, before, push_ps, range(STACKS))
             if t + AHEAD < TILES:
-                load_tile(t + AHEAD)
+                load_h(t + AHEAD)
+                load_stacks(t + AHEAD, 0, 1 if t + AHEAD == SIDE_TILE else 4)
+                if t + AHEAD == SIDE_TILE - 1:
+                    load_stacks(SIDE_TILE, PART_STACK, PART_STACK + 1)
             for n in (2, 3):
                 stay(t, acc, n)
-            if t == 0:
-                nc.scalar.copy(out=bias_col[:], in_=bias_ps[:, 0:STACKS])
-            if t < len(SIDE_STACKS):
-                make_diagonals(SIDE_STACKS[t])
+            if t in (1, 3):
+                make_diagonals(SIDE_STACKS[t // 2])
             if 2 <= t < 2 + len(units):
                 empty_side(*units[t - 2], side_ps)
             if 1 <= t < 1 + len(units):

@@ -30,6 +30,9 @@ SIDE_TILE = TILES - 1
 SIDE_STACKS = (2, 3)
 PART_STACK = 1
 PART_FIRST = 6
+FED = (3, 5, 6)
+FED_STACK = 0
+HELPED_STACK = 1
 AHEAD = 3
 
 FLOPS = 2 * B * H * STACKS * CELL
@@ -46,6 +49,7 @@ def tile_stackrnncore_pa_kernel(tc, h, act_logits, stacks, W_push_words, W_push_
         stage = ctx.enter_context(tc.tile_pool(name="stage", bufs=2))
         blend = ctx.enter_context(tc.tile_pool(name="blend", bufs=4))
         psum = ctx.enter_context(tc.psum_pool(name="psum", bufs=2))
+        psum_one = ctx.enter_context(tc.psum_pool(name="psum_one", bufs=1))
         psum_side = ctx.enter_context(tc.psum_pool(name="psum_side", bufs=2))
         ctx.enter_context(tc.manual_schedule())
 
@@ -163,7 +167,7 @@ def tile_stackrnncore_pa_kernel(tc, h, act_logits, stacks, W_push_words, W_push_
             h_codes = stage.tile([P, PASSES * P], U32, align_bytes=64)
             h_scales = stage.tile([P, PASSES * P], U8, align_bytes=64)
             nc.vector.quantize_mx(out=h_codes[:].bitcast(FP8X4), scales=h_scales[:], in_=grouped[:])
-            push_t_ps = psum.tile([P, STACKS, P], F32)
+            push_t_ps = psum_one.tile([P, STACKS, P], F32)
             for n in range(STACKS):
                 for g in range(PASSES):
                     nc.tensor.matmul_mx(
@@ -179,7 +183,7 @@ def tile_stackrnncore_pa_kernel(tc, h, act_logits, stacks, W_push_words, W_push_
 
         def add_bias_and_turn_back(push_t_ps):
             push_t = stage.tile([P, STACKS, P], F32)
-            push_ps = psum.tile([P, STACKS, CELL], F32)
+            push_ps = psum_one.tile([P, STACKS, CELL], F32)
             for n in range(STACKS):
                 nc.scalar.activation(
                     out=push_t[:, n, :], in_=push_t_ps[:, n, :], func=ACT.Identity, bias=bias_col[:, n : n + 1], scale=1.0
@@ -205,29 +209,65 @@ def tile_stackrnncore_pa_kernel(tc, h, act_logits, stacks, W_push_words, W_push_
                 op1=ALU.mult,
             )
 
-        def pop(t, acc, n, cells=CELLS):
+        def pop(t, acc, n, cells=CELLS, source=None):
             width = CELL * min(cells, CELLS - 1)
+            values = stack_sb[t][:, n, :] if source is None else source
             nc.vector.scalar_tensor_tensor(
                 out=acc[:, n, 0:width],
-                in0=stack_sb[t][:, n, CELL : CELL + width],
+                in0=values[:, CELL : CELL + width],
                 scalar=weight(t, n, 1),
                 in1=acc[:, n, 0:width],
                 op0=ALU.mult,
                 op1=ALU.add,
             )
 
-        def shift_down(t, acc, n, cells=CELLS, first=1):
+        def shift_down(t, acc, n, cells=CELLS, first=1, source=None):
             low = CELL * first
             width = CELL * cells
+            values = stack_sb[t][:, n, :] if source is None else source
             nc.vector.scalar_tensor_tensor(
                 out=acc[:, n, low:width],
-                in0=stack_sb[t][:, n, low - CELL : width - CELL],
+                in0=values[:, low - CELL : width - CELL],
                 scalar=weight(t, n, 0),
                 in1=acc[:, n, low:width],
                 op0=ALU.mult,
                 op1=ALU.add,
             )
-            nc.sync.dma_start(out=out_rows[:, t, n, low:width], in_=acc[:, n, low:width])
+            store(t, acc, n, first, cells)
+
+        def store(t, acc, n, first, end):
+            cells = slice(CELL * first, CELL * end)
+            nc.sync.dma_start(out=out_rows[:, t, n, cells], in_=acc[:, n, cells])
+
+        def turn_stack(t):
+            words = stack_sb[t][:, FED_STACK, :].bitcast(F32)
+            turned_stack_ps = psum_one.tile([P, DEPTH // 2 // P, P], F32)
+            for j in range(DEPTH // 2 // P):
+                nc.tensor.transpose(turned_stack_ps[:, j, :], words[:, P * j : P * (j + 1)], ident[:])
+            return turned_stack_ps
+
+        def copy_stack(turned_stack_ps):
+            turned_stack = stage.tile([P, DEPTH // 2 // P, P], F32)
+            nc.scalar.copy(out=turned_stack[:], in_=turned_stack_ps[:])
+            return turned_stack
+
+        def turn_stack_back(turned_stack):
+            fed_ps = psum_one.tile([P, DEPTH // 2], F32)
+            for j in range(DEPTH // 2 // P):
+                nc.tensor.transpose(fed_ps[:, P * j : P * (j + 1)], turned_stack[:, j, :], ident[:])
+            return fed_ps[:].bitcast(BF16)
+
+        def push_term(t):
+            term = stage.tile([P, DEPTH - CELL], F32)
+            nc.scalar.activation(
+                out=term[:], in_=stack_sb[t][:, HELPED_STACK, 0 : DEPTH - CELL], func=ACT.Copy, scale=weight(t, HELPED_STACK, 0)
+            )
+            return term
+
+        def add_push_term(t, acc, term):
+            cells = acc[:, HELPED_STACK, CELL:DEPTH]
+            nc.gpsimd.tensor_tensor(out=cells, in0=cells, in1=term[:], op=ALU.add)
+            store(t, acc, HELPED_STACK, 1, CELLS)
 
         def push_on_top(t, acc, n, push_ps):
             nc.vector.scalar_tensor_tensor(
@@ -300,6 +340,8 @@ def tile_stackrnncore_pa_kernel(tc, h, act_logits, stacks, W_push_words, W_push_
             nc.sync.dma_start(out=out_rows[:, SIDE_TILE, PART_STACK, first:DEPTH], in_=acc_side[:, PART_STACK, first:DEPTH])
 
         units = [(n, half) for n in SIDE_STACKS for half in (0, 1)]
+        BLENDS = {2: [0], 3: [1], 4: [2], 5: [3]}
+        PART_TILE = 6
 
         def finish_tops(t, acc, push_ps, order):
             for n in order:
@@ -325,24 +367,45 @@ def tile_stackrnncore_pa_kernel(tc, h, act_logits, stacks, W_push_words, W_push_
                 shift_down(t, acc, 1)
                 normalise(other_tiles)
             else:
-                for n in (0, 1):
-                    stay(t, acc, n)
+                fed = t in FED
+                if t + 1 in FED:
+                    turned_stack_ps = turn_stack(t + 1)
+                if fed:
+                    stay(t, acc, 1)
+                    stay(t, acc, 0)
+                    pop(t, acc, 1)
+                else:
+                    for n in (0, 1):
+                        stay(t, acc, n)
                 if t == 1:
                     grouped = copy_h(turned)
                     bias_ps = turn_bias()
                     nc.scalar.copy(out=bias_col[:], in_=bias_ps[:, 0:STACKS])
                 push_ps = add_bias_and_turn_back(before_push_t_ps)
-                for n in (0, 1):
-                    pop(t, acc, n)
+                if not fed:
+                    for n in (0, 1):
+                        pop(t, acc, n)
                 if t > 1:
                     grouped = copy_h(turned)
-                side_ps = blend_on_tensor(*units[t - 2]) if 2 <= t < 2 + len(units) else None
-                part_ps = blend_part_on_tensor() if t == 2 + len(units) else None
+                if fed:
+                    term = push_term(t)
+                if t + 1 in FED:
+                    turned_stack = copy_stack(turned_stack_ps)
+                side_ps = [blend_on_tensor(*units[u]) for u in BLENDS.get(t, ())]
+                part_ps = blend_part_on_tensor() if t == PART_TILE else None
                 push_t_ps = multiply(grouped)
                 turned = transpose_h(t + 1)
-                for n in (0, 1):
-                    shift_down(t, acc, n)
-                finish_tops(t - 1, before, push_ps, range(STACKS))
+                if fed:
+                    pop(t, acc, 0, source=fed_values)
+                    add_push_term(t, acc, term)
+                    finish_tops(t - 1, before, push_ps, range(STACKS))
+                    shift_down(t, acc, 0, source=fed_values)
+                else:
+                    for n in (0, 1):
+                        shift_down(t, acc, n)
+                    finish_tops(t - 1, before, push_ps, range(STACKS))
+                if t + 1 in FED:
+                    fed_values = turn_stack_back(turned_stack)
             if t + AHEAD < TILES:
                 load_h(t + AHEAD)
                 load_stacks(t + AHEAD, 0, 1 if t + AHEAD == SIDE_TILE else 4)
@@ -350,16 +413,16 @@ def tile_stackrnncore_pa_kernel(tc, h, act_logits, stacks, W_push_words, W_push_
                     load_stacks(SIDE_TILE, PART_STACK, PART_STACK + 1)
             for n in (2, 3):
                 stay(t, acc, n)
-            if t in (1, 3):
-                make_diagonals(SIDE_STACKS[t // 2])
-            if 2 <= t < 2 + len(units):
-                empty_side(*units[t - 2], side_ps)
-            if 1 <= t < 1 + len(units):
-                widen(*units[t - 1])
-            if t == 1 + len(units):
+            for u in BLENDS.get(t, ()):
+                empty_side(*units[u], side_ps.pop(0))
+            for u in BLENDS.get(t + 1, ()):
+                if units[u][1] == 0:
+                    make_diagonals(units[u][0])
+                widen(*units[u])
+            if t == PART_TILE - 1:
                 make_diagonals(PART_STACK)
                 widen_part()
-            if t == 2 + len(units):
+            if t == PART_TILE:
                 empty_part(part_ps)
             if t == SIDE_TILE - 1:
                 last_grouped = copy_h(turned)

@@ -33,6 +33,7 @@ PART_FIRST = 6
 FED = (3, 5, 6)
 FED_STACK = 0
 HELPED_STACK = 1
+WHOLE = 4
 AHEAD = 3
 
 FLOPS = 2 * B * H * STACKS * CELL
@@ -236,8 +237,9 @@ def tile_stackrnncore_pa_kernel(tc, h, act_logits, stacks, W_push_words, W_push_
             store(t, acc, n, first, cells)
 
         def store(t, acc, n, first, end):
-            cells = slice(CELL * first, CELL * end)
-            nc.sync.dma_start(out=out_rows[:, t, n, cells], in_=acc[:, n, cells])
+            if t >= WHOLE:
+                cells = slice(CELL * first, CELL * end)
+                nc.sync.dma_start(out=out_rows[:, t, n, cells], in_=acc[:, n, cells])
 
         def turn_stack(t):
             words = stack_sb[t][:, FED_STACK, :].bitcast(F32)
@@ -346,7 +348,10 @@ def tile_stackrnncore_pa_kernel(tc, h, act_logits, stacks, W_push_words, W_push_
         def finish_tops(t, acc, push_ps, order):
             for n in order:
                 push_on_top(t, acc, n, push_ps)
-            nc.sync.dma_start(out=out_rows[:, t, :, 0:CELL], in_=acc[:, :, 0:CELL])
+                if t < WHOLE and n % 2 == 1:
+                    nc.sync.dma_start(out=out_rows[:, t, n - 1 : n + 1, :], in_=acc[:, n - 1 : n + 1, :])
+            if t >= WHOLE:
+                nc.sync.dma_start(out=out_rows[:, t, :, 0:CELL], in_=acc[:, :, 0:CELL])
 
         for t in range(TILES - 1):
             if t > 0:

@@ -30,7 +30,7 @@ SIDE_TILE = TILES - 1
 SIDE_STACKS = (2, 3)
 PART_STACK = 1
 PART_FIRST = 6
-FED = (3, 5, 6)
+FED = (3, 6)
 FED_STACK = 0
 HELPED_STACK = 1
 WHOLE = 4
@@ -357,6 +357,11 @@ def tile_stackrnncore_pa_kernel(tc, h, act_logits, stacks, W_push_words, W_push_
             if t > 0:
                 before, before_push_t_ps = acc, push_t_ps
             acc = blend.tile([P, STACKS, DEPTH], F32)
+            if t + AHEAD < TILES:
+                load_h(t + AHEAD)
+                load_stacks(t + AHEAD, 0, 1 if t + AHEAD == SIDE_TILE else 4)
+                if t + AHEAD == SIDE_TILE - 1:
+                    load_stacks(SIDE_TILE, PART_STACK, PART_STACK + 1)
             if t == 0:
                 stay_on_vector(t, acc, 0)
                 normalise(first_tile)
@@ -411,11 +416,6 @@ def tile_stackrnncore_pa_kernel(tc, h, act_logits, stacks, W_push_words, W_push_
                     finish_tops(t - 1, before, push_ps, range(STACKS))
                 if t + 1 in FED:
                     fed_values = turn_stack_back(turned_stack)
-            if t + AHEAD < TILES:
-                load_h(t + AHEAD)
-                load_stacks(t + AHEAD, 0, 1 if t + AHEAD == SIDE_TILE else 4)
-                if t + AHEAD == SIDE_TILE - 1:
-                    load_stacks(SIDE_TILE, PART_STACK, PART_STACK + 1)
             for n in (2, 3):
                 stay(t, acc, n)
             for u in BLENDS.get(t, ()):
@@ -430,6 +430,7 @@ def tile_stackrnncore_pa_kernel(tc, h, act_logits, stacks, W_push_words, W_push_
             if t == PART_TILE:
                 empty_part(part_ps)
             if t == SIDE_TILE - 1:
+                stay(SIDE_TILE, acc_side, 0)
                 last_grouped = copy_h(turned)
             for n in (2, 3):
                 pop(t, acc, n)
@@ -437,7 +438,6 @@ def tile_stackrnncore_pa_kernel(tc, h, act_logits, stacks, W_push_words, W_push_
             if t == SIDE_TILE - 1:
                 push_ps = add_bias_and_turn_back(push_t_ps)
                 last_push_t_ps = multiply(last_grouped)
-                stay(SIDE_TILE, acc_side, 0)
                 pop(SIDE_TILE, acc_side, 0)
             shift_down(t, acc, 3)
 

@@ -30,7 +30,7 @@ SIDE_TILE = TILES - 1
 SIDE_STACKS = (2, 3)
 PART_STACK = 1
 PART_FIRST = 6
-FED = (3, 6)
+FED = (3, 5)
 FED_STACK = 0
 HELPED_STACK = 1
 WHOLE = 4
@@ -380,24 +380,22 @@ def tile_stackrnncore_pa_kernel(tc, h, act_logits, stacks, W_push_words, W_push_
                 fed = t in FED
                 if t + 1 in FED:
                     turned_stack_ps = turn_stack(t + 1)
-                if fed:
-                    stay(t, acc, 1)
-                    stay(t, acc, 0)
-                    pop(t, acc, 1)
-                else:
-                    for n in (0, 1):
-                        stay(t, acc, n)
+                for n in (2, 1) if fed else (0, 1):
+                    stay(t, acc, n)
                 if t == 1:
                     grouped = copy_h(turned)
                     bias_ps = turn_bias()
                     nc.scalar.copy(out=bias_col[:], in_=bias_ps[:, 0:STACKS])
                 push_ps = add_bias_and_turn_back(before_push_t_ps)
-                if not fed:
+                if fed:
+                    pop(t, acc, 2)
+                else:
                     for n in (0, 1):
                         pop(t, acc, n)
                 if t > 1:
                     grouped = copy_h(turned)
                 if fed:
+                    stay(t, acc, 0)
                     term = push_term(t)
                 if t + 1 in FED:
                     turned_stack = copy_stack(turned_stack_ps)
@@ -406,6 +404,7 @@ def tile_stackrnncore_pa_kernel(tc, h, act_logits, stacks, W_push_words, W_push_
                 push_t_ps = multiply(grouped)
                 turned = transpose_h(t + 1)
                 if fed:
+                    pop(t, acc, 1)
                     pop(t, acc, 0, source=fed_values)
                     add_push_term(t, acc, term)
                     finish_tops(t - 1, before, push_ps, range(STACKS))
@@ -416,7 +415,8 @@ def tile_stackrnncore_pa_kernel(tc, h, act_logits, stacks, W_push_words, W_push_
                     finish_tops(t - 1, before, push_ps, range(STACKS))
                 if t + 1 in FED:
                     fed_values = turn_stack_back(turned_stack)
-            for n in (2, 3):
+            rest = (3,) if t in FED else (2, 3)
+            for n in rest:
                 stay(t, acc, n)
             for u in BLENDS.get(t, ()):
                 empty_side(*units[u], side_ps.pop(0))
@@ -432,7 +432,7 @@ def tile_stackrnncore_pa_kernel(tc, h, act_logits, stacks, W_push_words, W_push_
             if t == SIDE_TILE - 1:
                 stay(SIDE_TILE, acc_side, 0)
                 last_grouped = copy_h(turned)
-            for n in (2, 3):
+            for n in rest:
                 pop(t, acc, n)
             shift_down(t, acc, 2)
             if t == SIDE_TILE - 1:

from contextlib import ExitStack

import concourse.mybir as mybir
from concourse.masks import make_identity

F32 = mybir.dt.float32
BF16 = mybir.dt.bfloat16
U8 = mybir.dt.uint8
U32 = mybir.dt.uint32
I32 = mybir.dt.int32
FP8X4 = mybir.dt.float8_e4m3fn_x4
FP4X4 = mybir.dt.float4_e2m1fn_x4
ACT = mybir.ActivationFunctionType
ALU = mybir.AluOpType
AXIS_X = mybir.AxisListType.X

P = 128
B = 1024
H = 2048
STACKS = 4
CELLS = 8
CELL = 128
ACTIONS = 3
DEPTH = CELLS * CELL
TILES = B // P
PASSES = H // 512
WORDS = 256
BANK = 512
SIDE_TILE = TILES - 1
SIDE_STACKS = (2, 3)
PART_STACK = 1
PART_FIRST = 6
FED = (3, 5)
FED_STACK = 0
HELPED_STACK = 1
WHOLE = 4
AHEAD = 3

FLOPS = 2 * B * H * STACKS * CELL


def tile_stackrnncore_pa_kernel(tc, h, act_logits, stacks, W_push_words, W_push_scales, b_push, out):
    nc = tc.nc
    h_rows = h.rearrange("(p t) k -> p t k", t=TILES)
    stack_rows = stacks.rearrange("(p t) n i c -> p t n (i c)", t=TILES)
    out_rows = out.rearrange("(p t) n i c -> p t n (i c)", t=TILES)

    with ExitStack() as ctx:
        keep = ctx.enter_context(tc.tile_pool(name="keep", bufs=1))
        stage = ctx.enter_context(tc.tile_pool(name="stage", bufs=2))
        blend = ctx.enter_context(tc.tile_pool(name="blend", bufs=4))
        psum = ctx.enter_context(tc.psum_pool(name="psum", bufs=2))
        psum_one = ctx.enter_context(tc.psum_pool(name="psum_one", bufs=1))
        psum_side = ctx.enter_context(tc.psum_pool(name="psum_side", bufs=2))
        ctx.enter_context(tc.manual_schedule())

        zero = keep.tile([P, 1], F32)
        nc.gpsimd.memset(zero[:], 0.0)
        one = keep.tile([P, 1], F32)
        nc.scalar.activation(out=one[:], in_=zero[:], func=ACT.Exp)
        bias_rows = keep.tile([P, P], BF16)
        nc.gpsimd.memset(bias_rows[:], 0.0)
        ident = keep.tile([P, P], F32)
        make_identity(nc, ident[:])
        w_scales = keep.tile([P, PASSES, STACKS * CELL], U8, align_bytes=64)
        nc.vector.memset(w_scales[:].bitcast(I32), 0)

        logits = keep.tile([P, TILES, STACKS * ACTIONS], BF16)
        nc.sync.dma_start(out=logits[:], in_=act_logits.rearrange("(p t) a -> p t a", t=TILES))
        stack_sb = [keep.tile([P, STACKS, DEPTH], BF16, name="stack_sb%d" % t) for t in range(TILES)]
        h_sb = [keep.tile([P, H], BF16, name="h_sb%d" % t) for t in range(TILES)]
        w_words = keep.tile([P, PASSES, 2 * STACKS * CELL], U8, align_bytes=64)
        scale_words = W_push_scales.bitcast(I32)

        def load_h(t):
            nc.sync.dma_start(out=h_sb[t][:], in_=h_rows[:, t, :])

        def load_stacks(t, first=0, end=STACKS):
            nc.sync.dma_start(out=stack_sb[t][:, first:end, :], in_=stack_rows[:, t, first:end, :])

        def load_weight():
            for quad in range(4):
                nc.sync.dma_start(
                    out=w_scales[32 * quad : 32 * quad + 4, :, :].bitcast(I32),
                    in_=scale_words[:, 4 * quad : 4 * quad + 4, :].rearrange("g r w -> r g w"),
                )
            nc.sync.dma_start(out=w_words[:].bitcast(I32), in_=W_push_words.bitcast(I32).rearrange("g p w -> p g w"))
            nc.sync.dma_start(out=bias_rows[0:STACKS, :], in_=b_push.rearrange("(n c) -> n c", n=STACKS))

        load_stacks(0, 0, 1)
        load_stacks(0, 1, 2)
        load_h(0)
        load_stacks(0, 2, 4)
        load_stacks(1, 0, 2)
        load_weight()
        load_h(1)
        load_stacks(1, 2, 4)
        load_h(2)
        load_stacks(2)
        load_stacks(SIDE_TILE, 2, 4)

        shape = [P, TILES, STACKS * ACTIONS]
        minus_top = keep.tile([P, TILES], F32)
        nc.vector.tensor_reduce(out=minus_top[:], in_=logits[:], axis=AXIS_X, op=ALU.max, negate=True)
        expd = keep.tile(shape, F32)
        total = keep.tile([P, TILES], F32)
        inverse = keep.tile([P, TILES], F32)
        weights = keep.tile(shape, F32)

        def exponentials(tiles):
            for t in tiles:
                nc.scalar.activation(
                    out=expd[:, t, :],
                    in_=logits[:, t, :],
                    func=ACT.Exp,
                    bias=minus_top[:, t : t + 1],
                    scale=1.0,
                    accum_out=total[:, t : t + 1],
                )

        def invert_totals(tiles):
            nc.vector.reciprocal(out=inverse[:, tiles], in_=total[:, tiles])

        def normalise(tiles):
            nc.vector.tensor_tensor(
                out=weights[:, tiles, :],
                in0=expd[:, tiles, :],
                in1=inverse[:, tiles].unsqueeze(2).to_broadcast([P, tiles.stop - tiles.start, STACKS * ACTIONS]),
                op=ALU.mult,
            )

        first_tile = slice(0, 1)
        other_tiles = slice(1, TILES)
        exponentials(range(0, 1))
        invert_totals(first_tile)

        def weight(t, n, action):
            column = ACTIONS * n + action
            return weights[:, t, column : column + 1]

        def transpose_h(t):
            h_words = h_sb[t][:].bitcast(F32)
            turned = []
            for half in range(2):
                turned_ps = psum.tile([P, 4, P], F32)
                for g in range(2):
                    for u in range(2):
                        k_pass = 2 * half + g
                        nc.tensor.transpose(
                            turned_ps[:, 2 * g + u, :],
                            h_words[:, WORDS * k_pass + u : WORDS * (k_pass + 1) : 2],
                            ident[:],
                        )
                turned.append(turned_ps)
            return turned

        def copy_h(turned):
            grouped = stage.tile([P, H], BF16, align_bytes=64)
            grouped_words = grouped[:].bitcast(F32).rearrange("p (g b u) -> p g b u", g=PASSES, u=2)
            for half in range(2):
                nc.scalar.copy(
                    out=grouped_words[:, 2 * half : 2 * half + 2, :, :],
                    in_=turned[half][:].rearrange("p (g u) b -> p g b u", u=2),
                )
            return grouped

        def multiply(grouped):
            h_codes = stage.tile([P, PASSES * P], U32, align_bytes=64)
            h_scales = stage.tile([P, PASSES * P], U8, align_bytes=64)
            nc.vector.quantize_mx(out=h_codes[:].bitcast(FP8X4), scales=h_scales[:], in_=grouped[:])
            push_t_ps = psum_one.tile([P, STACKS, P], F32)
            for n in range(STACKS):
                for g in range(PASSES):
                    nc.tensor.matmul_mx(
                        out=push_t_ps[:, n, :],
                        lhsT=w_words[:, g, 2 * CELL * n : 2 * CELL * (n + 1)].bitcast(FP4X4),
                        lhsT_scale=w_scales[:, g, CELL * n : CELL * (n + 1)],
                        rhs=h_codes[:, P * g : P * (g + 1)].bitcast(FP8X4),
                        rhs_scale=h_scales[:, P * g : P * (g + 1)],
                        start=(g == 0),
                        stop=(g == PASSES - 1),
                    )
            return push_t_ps

        def add_bias_and_turn_back(push_t_ps):
            push_t = stage.tile([P, STACKS, P], F32)
            push_ps = psum_one.tile([P, STACKS, CELL], F32)
            for n in range(STACKS):
                nc.scalar.activation(
                    out=push_t[:, n, :], in_=push_t_ps[:, n, :], func=ACT.Identity, bias=bias_col[:, n : n + 1], scale=1.0
                )
            for n in range(STACKS):
                nc.tensor.transpose(push_ps[:, n, :], push_t[:, n, :], ident[:])
            return push_ps

        def stay(t, acc, n, cells=CELLS):
            width = CELL * cells
            nc.scalar.activation(
                out=acc[:, n, 0:width], in_=stack_sb[t][:, n, 0:width], func=ACT.Copy, scale=weight(t, n, 2)
            )

        def stay_on_vector(t, acc, n):
            column = ACTIONS * n + 2
            nc.vector.tensor_scalar(
                out=acc[:, n, :],
                in0=stack_sb[t][:, n, :],
                scalar1=expd[:, t, column : column + 1],
                scalar2=inverse[:, t : t + 1],
                op0=ALU.mult,
                op1=ALU.mult,
            )

        def pop(t, acc, n, cells=CELLS, source=None):
            width = CELL * min(cells, CELLS - 1)
            values = stack_sb[t][:, n, :] if source is None else source
            nc.vector.scalar_tensor_tensor(
                out=acc[:, n, 0:width],
                in0=values[:, CELL : CELL + width],
                scalar=weight(t, n, 1),
                in1=acc[:, n, 0:width],
                op0=ALU.mult,
                op1=ALU.add,
            )

        def shift_down(t, acc, n, cells=CELLS, first=1, source=None):
            low = CELL * first
            width = CELL * cells
            values = stack_sb[t][:, n, :] if source is None else source
            nc.vector.scalar_tensor_tensor(
                out=acc[:, n, low:width],
                in0=values[:, low - CELL : width - CELL],
                scalar=weight(t, n, 0),
                in1=acc[:, n, low:width],
                op0=ALU.mult,
                op1=ALU.add,
            )
            store(t, acc, n, first, cells)

        def store(t, acc, n, first, end):
            if t >= WHOLE:
                cells = slice(CELL * first, CELL * end)
                nc.sync.dma_start(out=out_rows[:, t, n, cells], in_=acc[:, n, cells])

        def turn_stack(t):
            words = stack_sb[t][:, FED_STACK, :].bitcast(F32)
            turned_stack_ps = psum_one.tile([P, DEPTH // 2 // P, P], F32)
            for j in range(DEPTH // 2 // P):
                nc.tensor.transpose(turned_stack_ps[:, j, :], words[:, P * j : P * (j + 1)], ident[:])
            return turned_stack_ps

        def copy_stack(turned_stack_ps):
            turned_stack = stage.tile([P, DEPTH // 2 // P, P], F32)
            nc.scalar.copy(out=turned_stack[:], in_=turned_stack_ps[:])
            return turned_stack

        def turn_stack_back(turned_stack):
            fed_ps = psum_one.tile([P, DEPTH // 2], F32)
            for j in range(DEPTH // 2 // P):
                nc.tensor.transpose(fed_ps[:, P * j : P * (j + 1)], turned_stack[:, j, :], ident[:])
            return fed_ps[:].bitcast(BF16)

        def push_term(t):
            term = stage.tile([P, DEPTH - CELL], F32)
            nc.scalar.activation(
                out=term[:], in_=stack_sb[t][:, HELPED_STACK, 0 : DEPTH - CELL], func=ACT.Copy, scale=weight(t, HELPED_STACK, 0)
            )
            return term

        def add_push_term(t, acc, term):
            cells = acc[:, HELPED_STACK, CELL:DEPTH]
            nc.gpsimd.tensor_tensor(out=cells, in0=cells, in1=term[:], op=ALU.add)
            store(t, acc, HELPED_STACK, 1, CELLS)

        def push_on_top(t, acc, n, push_ps):
            nc.vector.scalar_tensor_tensor(
                out=acc[:, n, 0:CELL],
                in0=push_ps[:, n, :],
                scalar=weight(t, n, 0),
                in1=acc[:, n, 0:CELL],
                op0=ALU.mult,
                op1=ALU.add,
            )

        bias_col = keep.tile([P, STACKS], F32)

        def turn_bias():
            bias_rows_f32 = keep.tile([P, P], F32)
            nc.scalar.copy(out=bias_rows_f32[:], in_=bias_rows[:])
            bias_ps = psum_side.tile([P, P], F32, tag="side")
            nc.tensor.transpose(bias_ps[:], bias_rows_f32[:], ident[:])
            return bias_ps

        acc_side = keep.tile([P, STACKS, DEPTH], F32)
        wide = {n: keep.tile([P, DEPTH], F32, name="wide%d" % n) for n in SIDE_STACKS + (PART_STACK,)}
        diag = {}

        def make_diagonals(n):
            for action in range(ACTIONS):
                diag[(n, action)] = keep.tile([P, P], F32, name="diag%d_%d" % (n, action))
                nc.scalar.activation(
                    out=diag[(n, action)][:], in_=ident[:], func=ACT.Copy, scale=weight(SIDE_TILE, n, action)
                )

        def widen(n, half):
            columns = slice(0, 5 * CELL) if half == 0 else slice(5 * CELL, DEPTH)
            nc.scalar.copy(out=wide[n][:, columns], in_=stack_sb[SIDE_TILE][:, n, columns])

        def blend_on_tensor(n, half):
            side_ps = psum_side.tile([P, BANK], F32, tag="side")
            first = BANK * half
            nc.tensor.matmul(side_ps[:], lhsT=diag[(n, 2)][:], rhs=wide[n][:, first : first + BANK], start=True, stop=False)
            if half == 0:
                nc.tensor.matmul(side_ps[:], lhsT=diag[(n, 1)][:], rhs=wide[n][:, CELL : CELL + BANK], start=False, stop=False)
                nc.tensor.matmul(side_ps[:, CELL:BANK], lhsT=diag[(n, 0)][:], rhs=wide[n][:, 0 : BANK - CELL], start=False, stop=True)
            else:
                nc.tensor.matmul(side_ps[:], lhsT=diag[(n, 0)][:], rhs=wide[n][:, BANK - CELL : DEPTH - CELL], start=False, stop=False)
                nc.tensor.matmul(side_ps[:, 0 : BANK - CELL], lhsT=diag[(n, 1)][:], rhs=wide[n][:, BANK + CELL : DEPTH], start=False, stop=True)
            return side_ps

        def empty_side(n, half, side_ps):
            nc.scalar.copy(out=acc_side[:, n, BANK * half : BANK * (half + 1)], in_=side_ps[:])
            if half == 1:
                nc.sync.dma_start(out=out_rows[:, SIDE_TILE, n, CELL:DEPTH], in_=acc_side[:, n, CELL:DEPTH])

        def widen_part():
            columns = slice(CELL * (PART_FIRST - 1), DEPTH)
            nc.scalar.copy(out=wide[PART_STACK][:, columns], in_=stack_sb[SIDE_TILE][:, PART_STACK, columns])

        def blend_part_on_tensor():
            n = PART_STACK
            first = CELL * PART_FIRST
            width = DEPTH - first
            part_ps = psum_side.tile([P, BANK], F32, tag="side")
            nc.tensor.matmul(part_ps[:, 0:width], lhsT=diag[(n, 2)][:], rhs=wide[n][:, first:DEPTH], start=True, stop=False)
            nc.tensor.matmul(part_ps[:, 0:width], lhsT=diag[(n, 0)][:], rhs=wide[n][:, first - CELL : DEPTH - CELL], start=False, stop=False)
            nc.tensor.matmul(part_ps[:, 0 : width - CELL], lhsT=diag[(n, 1)][:], rhs=wide[n][:, first + CELL : DEPTH], start=False, stop=True)
            return part_ps

        def empty_part(part_ps):
            first = CELL * PART_FIRST
            nc.scalar.copy(out=acc_side[:, PART_STACK, first:DEPTH], in_=part_ps[:, 0 : DEPTH - first])
            nc.sync.dma_start(out=out_rows[:, SIDE_TILE, PART_STACK, first:DEPTH], in_=acc_side[:, PART_STACK, first:DEPTH])

        units = [(n, half) for n in SIDE_STACKS for half in (0, 1)]
        BLENDS = {2: [0], 3: [1], 4: [2], 5: [3]}
        PART_TILE = 6

        def finish_tops(t, acc, push_ps, order):
            for n in order:
                push_on_top(t, acc, n, push_ps)
                if t < WHOLE and n % 2 == 1:
                    nc.sync.dma_start(out=out_rows[:, t, n - 1 : n + 1, :], in_=acc[:, n - 1 : n + 1, :])
            if t >= WHOLE:
                nc.sync.dma_start(out=out_rows[:, t, :, 0:CELL], in_=acc[:, :, 0:CELL])

        for t in range(TILES - 1):
            if t > 0:
                before, before_push_t_ps = acc, push_t_ps
            acc = blend.tile([P, STACKS, DEPTH], F32)
            if t + AHEAD < TILES:
                load_h(t + AHEAD)
                load_stacks(t + AHEAD, 0, 1 if t + AHEAD == SIDE_TILE else 4)
                if t + AHEAD == SIDE_TILE - 1:
                    load_stacks(SIDE_TILE, PART_STACK, PART_STACK + 1)
            if t == 0:
                stay_on_vector(t, acc, 0)
                normalise(first_tile)
                stay_on_vector(t, acc, 1)
                for n in (0, 1):
                    pop(t, acc, n)
                grouped = copy_h(transpose_h(t))
                exponentials(range(1, TILES))
                shift_down(t, acc, 0)
                push_t_ps = multiply(grouped)
                turned = transpose_h(1)
                invert_totals(other_tiles)
                shift_down(t, acc, 1)
                normalise(other_tiles)
            else:
                fed = t in FED
                if t + 1 in FED:
                    turned_stack_ps = turn_stack(t + 1)
                for n in (2, 1) if fed else (0, 1):
                    stay(t, acc, n)
                if t == 1:
                    grouped = copy_h(turned)
                    bias_ps = turn_bias()
                    nc.scalar.copy(out=bias_col[:], in_=bias_ps[:, 0:STACKS])
                push_ps = add_bias_and_turn_back(before_push_t_ps)
                if fed:
                    pop(t, acc, 2)
                else:
                    for n in (0, 1):
                        pop(t, acc, n)
                if t > 1:
                    grouped = copy_h(turned)
                if fed:
                    stay(t, acc, 0)
                    term = push_term(t)
                if t + 1 in FED:
                    turned_stack = copy_stack(turned_stack_ps)
                side_ps = [blend_on_tensor(*units[u]) for u in BLENDS.get(t, ())]
                part_ps = blend_part_on_tensor() if t == PART_TILE else None
                push_t_ps = multiply(grouped)
                turned = transpose_h(t + 1)
                if fed:
                    pop(t, acc, 1)
                    pop(t, acc, 0, source=fed_values)
                    add_push_term(t, acc, term)
                    finish_tops(t - 1, before, push_ps, range(STACKS))
                    shift_down(t, acc, 0, source=fed_values)
                else:
                    for n in (0, 1):
                        shift_down(t, acc, n)
                    finish_tops(t - 1, before, push_ps, range(STACKS))
                if t + 1 in FED:
                    fed_values = turn_stack_back(turned_stack)
            rest = (3,) if t in FED else (2, 3)
            for n in rest:
                stay(t, acc, n)
            for u in BLENDS.get(t, ()):
                empty_side(*units[u], side_ps.pop(0))
            for u in BLENDS.get(t + 1, ()):
                if units[u][1] == 0:
                    make_diagonals(units[u][0])
                widen(*units[u])
            if t == PART_TILE - 1:
                make_diagonals(PART_STACK)
                widen_part()
            if t == PART_TILE:
                empty_part(part_ps)
            if t == SIDE_TILE - 1:
                stay(SIDE_TILE, acc_side, 0)
                last_grouped = copy_h(turned)
            for n in rest:
                pop(t, acc, n)
            shift_down(t, acc, 2)
            if t == SIDE_TILE - 1:
                push_ps = add_bias_and_turn_back(push_t_ps)
                last_push_t_ps = multiply(last_grouped)
                pop(SIDE_TILE, acc_side, 0)
            shift_down(t, acc, 3)

        t = SIDE_TILE
        mine = {0: CELLS, PART_STACK: PART_FIRST}
        finish_tops(t - 1, acc, push_ps, range(STACKS))
        stay(t, acc_side, 1, mine[1])
        last_push_ps = add_bias_and_turn_back(last_push_t_ps)
        shift_down(t, acc_side, 0, mine[0])
        pop(t, acc_side, 1, mine[1])
        finish_tops(t, acc_side, last_push_ps, (2, 3, 0, 1))
        shift_down(t, acc_side, 1, 4)
        shift_down(t, acc_side, 1, mine[1], 4)
